import numpy as np
import ml_dtypes


def mxq(x, axis, fmt="e4m3"):
    dtype, down = {"e4m3": (ml_dtypes.float8_e4m3fn, 7), "e5m2": (ml_dtypes.float8_e5m2, 14)}[fmt]
    v = np.moveaxis(np.asarray(x, np.float32).astype(ml_dtypes.bfloat16).astype(np.float64), axis, -1)
    blocks = v.reshape(v.shape[:-1] + (-1, 32))
    amax = np.abs(blocks).max(-1, keepdims=True)
    byte = np.maximum(np.where(amax > 0, np.frexp(amax)[1] - 1 + 127, 0) - down, 1)
    scale = np.exp2(byte - 127.0)
    codes = (blocks / scale).astype(np.float32).astype(dtype).astype(np.float64)
    return np.moveaxis((codes * scale).reshape(v.shape), -1, axis)


WIDE = False


def mx_kscale(k):
    if not WIDE:
        return np.ones(k)
    levels = np.array([10, -10, 5, -5, 0])
    a = np.random.permutation(np.resize(levels, k // 512 * 4)).reshape(k // 512, 4)
    idx = np.arange(k)
    return np.exp2(a[idx // 512, idx % 128 // 32])


BF16 = ml_dtypes.bfloat16


def bf(x):
    return np.asarray(x, np.float32).astype(BF16)


def f64(x):
    return np.asarray(x).astype(np.float64)


S, B, D, H, DH = 512, 8, 1024, 4, 128


def setup_inputs():
    s = mx_kscale(D)
    return {"q": bf(np.random.standard_normal((B, H, S, DH))),
            "k": bf(np.random.standard_normal((B, H, S, DH))),
            "x": bf(np.random.standard_normal((S, B, D)) * s),
            "wv": bf(np.random.standard_normal((H, DH, D)) * 3.0 / np.sqrt(D) / s),
            "mask": bf(np.random.uniform(size=(B, S)) > 0.2)}


def reference(q, k, x, wv, mask):
    v = mxq(f64(x), 2, "e4m3").reshape(S * B, D) @ mxq(f64(wv), 2, "e4m3").reshape(H * DH, D).T
    v = v.reshape(S, B, H, DH).transpose(1, 2, 0, 3)
    sc = f64(q) @ f64(k).transpose(0, 1, 3, 2)
    a = np.tanh(sc / np.sqrt(DH)) - 10000.0 * (1.0 - f64(mask))[:, None, None, :]
    e = np.exp(a - a.max(-1, keepdims=True))
    o = (mxq(e, 3, "e4m3") @ mxq(v, 2, "e4m3")) / e.sum(-1, keepdims=True)
    return o.transpose(2, 0, 1, 3).reshape(S, B, H * DH)

@@ -1,0 +1,336 @@
+from contextlib import ExitStack
+import math
+
+import concourse.mybir as mybir
+from concourse.masks import make_identity
+
+F32 = mybir.dt.float32
+BF16 = mybir.dt.bfloat16
+U32 = mybir.dt.uint32
+U8 = mybir.dt.uint8
+FP8X4 = mybir.dt.float8_e4m3fn_x4
+ACT = mybir.ActivationFunctionType
+ALU = mybir.AluOpType
+
+S, B, D, H, DH = 512, 8, 1024, 4, 128
+P = 128
+CHUNKS = S // P
+K_PASS = 512
+PASSES = D // K_PASS
+STEPS = B * H
+
+FLOPS = 2 * S * B * D * H * DH + 2 * 2 * B * H * S * S * DH
+
+QK_LEAD = 3
+X_LEAD = 2
+V_LAG = 4 - X_LEAD
+DMA_LEAD = 4
+
+
+def tile_attention_pa_t_kernel(tc, q, k, x, wv, mask, out):
+    nc = tc.nc
+    with ExitStack() as stack:
+        pool = lambda name, bufs: stack.enter_context(tc.tile_pool(name=name, bufs=bufs))
+        psum = lambda name, bufs: stack.enter_context(tc.psum_pool(name=name, bufs=bufs))
+        const = pool("const", 1)
+        raw = pool("raw", 2)
+        proj = pool("proj", 2)
+        qk_pool = pool("qk", QK_LEAD + 1)
+        soft = pool("soft", 3)
+        kept = pool("kept", V_LAG + 4)
+        val = pool("val", 3)
+        res = pool("res", 2)
+        ps_s = psum("ps_s", 2)
+        ps_et = psum("ps_et", 2)
+        ps_one = psum("ps_one", 1)
+
+        ident_f32 = const.tile([P, P], F32)
+        make_identity(nc, ident_f32[:])
+        ident_bf = const.tile([P, P], BF16)
+        make_identity(nc, ident_bf[:])
+        mask_all = const.tile([P, B * S], BF16)
+        nc.scalar.dma_start(out=mask_all[:], in_=mask.rearrange("b t -> (b t)").partition_broadcast(P))
+        mask_term = const.tile([P, B * S], F32)
+        nc.vector.tensor_scalar(
+            out=mask_term[:], in0=mask_all[:], scalar1=10000.0, scalar2=-10000.0, op0=ALU.mult, op1=ALU.add
+        )
+
+        live = {}
+
+        def transpose_piece(rows_sb, piece):
+            g, pair = divmod(piece, 2)
+            words = rows_sb[:].bitcast(F32)
+            xt = ps_one.tile([P, 512], F32)
+            for u in range(2):
+                for s in range(2):
+                    first = (2 * pair + s) * (D // 2) + (2 * g + u) * P
+                    nc.tensor.transpose(
+                        xt[:, (2 * u + s) * P : (2 * u + s + 1) * P], words[:, first : first + P], ident_f32[:]
+                    )
+            return xt
+
+        def regroup_piece(xt, piece, grouped):
+            g, pair = divmod(piece, 2)
+            words = grouped[:].bitcast(F32).rearrange("p (g c u) -> p g c u", g=PASSES, u=2)
+            nc.vector.tensor_copy(
+                out=words[:, g, 256 * pair : 256 * (pair + 1), :], in_=xt[:].rearrange("p (u c) -> p c u", u=2)
+            )
+
+        def quantise_pass(grouped, g, codes, scales):
+            cols = slice(g * S, (g + 1) * S)
+            nc.vector.quantize_mx(
+                out=codes[:, cols].bitcast(FP8X4),
+                scales=scales[:, cols],
+                in_=grouped[:, g * 4 * S : (g + 1) * 4 * S],
+            )
+
+        w_codes = const.tile([P, PASSES * S], U32, align_bytes=64)
+        w_scales = const.tile([P, PASSES * S], U8, align_bytes=64)
+
+        def load_qk(b):
+            q_sb = raw.tile([P, H * S], BF16)
+            nc.sync.dma_start(
+                out=q_sb[:].rearrange("p (h f) -> p h f", h=H), in_=q[b].rearrange("h (p a) c -> p h (a c)", a=CHUNKS)
+            )
+            k_sb = raw.tile([P, H * S], BF16)
+            nc.sync.dma_start(
+                out=k_sb[:].rearrange("p (f c) -> p f c", c=DH), in_=k[b].rearrange("h (a p) c -> p (h a) c", p=P)
+            )
+            live["q_sb", b], live["k_sb", b] = q_sb, k_sb
+
+        def load_rows(b):
+            x_sb = raw.tile([P, CHUNKS * D], BF16)
+            slabs = x_sb[:].rearrange("p (j d) -> p j d", j=CHUNKS)
+            if b < 0:
+                nc.sync.dma_start(out=slabs, in_=wv.rearrange("h c d -> c h d"))
+            else:
+                rows = x[:, b, :].rearrange("(u p e) d -> u p e d", u=2, e=2)
+                for u in range(2):
+                    nc.sync.dma_start(out=slabs[:, 2 * u : 2 * u + 2, :], in_=rows[u])
+            live["x_sb", b] = x_sb
+
+        def transpose_qk(n):
+            b, h = divmod(n, H)
+            qkt = ps_one.tile([P, 2 * S], BF16)
+            for which, rows_sb in enumerate((live["q_sb", b], live["k_sb", b])):
+                for a in range(CHUNKS):
+                    nc.tensor.transpose(
+                        qkt[:, which * S + a * P : which * S + (a + 1) * P],
+                        rows_sb[:, (h * CHUNKS + a) * DH : (h * CHUNKS + a + 1) * DH],
+                        ident_bf[:],
+                    )
+            live["qkt", n] = qkt
+
+        def transpose_x(slot):
+            b, h = divmod(slot, H)
+            live["xt", slot] = transpose_piece(live["x_sb", b], h)
+
+        def regroup_x(slot):
+            b, h = divmod(slot, H)
+            if h == 0:
+                x_grouped = proj.tile([P, PASSES * 4 * S], BF16, align_bytes=64)
+                live["x_grouped", b] = x_grouped
+                if b < 0:
+                    live["x_codes", b], live["x_scales", b] = w_codes, w_scales
+                else:
+                    x_codes = proj.tile([P, PASSES * S], U32, align_bytes=64)
+                    x_scales = proj.tile([P, PASSES * S], U8, align_bytes=64)
+                    live["x_codes", b], live["x_scales", b] = x_codes, x_scales
+            regroup_piece(live["xt", slot], h, live["x_grouped", b])
+
+        def quantise_x(slot):
+            b, h = divmod(slot, H)
+            if h % 2 == 1:
+                quantise_pass(live["x_grouped", b], h // 2, live["x_codes", b], live["x_scales", b])
+
+        def copy_qk(n):
+            qk_t = qk_pool.tile([P, 2 * S], BF16)
+            nc.scalar.copy(out=qk_t[:], in_=live["qkt", n][:])
+            live["qk_t", n] = qk_t
+
+        def scores(chunk):
+            n, a = divmod(chunk, CHUNKS)
+            qk_t = live["qk_t", n]
+            s_ps = ps_s.tile([P, S], F32)
+            nc.tensor.matmul(s_ps[:], lhsT=qk_t[:, a * P : (a + 1) * P], rhs=qk_t[:, S : 2 * S], start=True, stop=True)
+            live["s_ps", chunk] = s_ps
+
+        def squash(n, a):
+            if a == 0:
+                att = soft.tile([P, CHUNKS * S], F32)
+                live["att", n] = att
+            nc.scalar.activation(
+                out=live["att", n][:, a * S : (a + 1) * S],
+                in_=live["s_ps", n * CHUNKS + a][:],
+                func=ACT.Tanh,
+                scale=1.0 / math.sqrt(DH),
+            )
+
+        def add_mask(n, a):
+            b = n // H
+            chunk = live["att", n][:, a * S : (a + 1) * S]
+            nc.gpsimd.tensor_tensor(out=chunk, in0=chunk, in1=mask_term[:, b * S : (b + 1) * S], op=ALU.add)
+
+        def project_v(n):
+            b, h = divmod(n, H)
+            v_ps = ps_one.tile([P, CHUNKS * DH], F32)
+            for j in range(CHUNKS):
+                for g in range(PASSES):
+                    rows = slice(g * S + j * P, g * S + (j + 1) * P)
+                    cols = slice(g * S + h * DH, g * S + (h + 1) * DH)
+                    nc.tensor.matmul_mx(
+                        out=v_ps[:, j * DH : (j + 1) * DH],
+                        lhsT=live["x_codes", b][:, rows].bitcast(FP8X4),
+                        lhsT_scale=live["x_scales", b][:, rows],
+                        rhs=w_codes[:, cols].bitcast(FP8X4),
+                        rhs_scale=w_scales[:, cols],
+                        start=(g == 0),
+                        stop=(g == PASSES - 1),
+                    )
+            live["v_ps", n] = v_ps
+
+        def regroup_v(n):
+            v_grouped = val.tile([P, 4 * DH], BF16, align_bytes=64)
+            nc.vector.tensor_copy(
+                out=v_grouped[:].rearrange("p (c j) -> p c j", j=4),
+                in_=live["v_ps", n][:].rearrange("p (j c) -> p c j", j=4),
+            )
+            live["v_grouped", n] = v_grouped
+
+        def quantise_v(n):
+            v_codes = val.tile([P, DH], U32, align_bytes=64)
+            v_scales = val.tile([P, DH], U8, align_bytes=64)
+            nc.vector.quantize_mx(out=v_codes[:].bitcast(FP8X4), scales=v_scales[:], in_=live["v_grouped", n][:])
+            live["v_codes", n], live["v_scales", n] = v_codes, v_scales
+
+        def row_max(n, pair):
+            if pair == 0:
+                neg_max = soft.tile([P, CHUNKS], F32)
+                live["neg_max", n] = neg_max
+            att = live["att", n][:].rearrange("p (a t) -> p a t", a=CHUNKS)
+            two = slice(2 * pair, 2 * pair + 2)
+            nc.vector.tensor_reduce(
+                out=live["neg_max", n][:, two], in_=att[:, two, :], axis=mybir.AxisListType.X, op=ALU.max, negate=True
+            )
+
+        def exp_and_transpose(n):
+            e_sb = soft.tile([P, CHUNKS * S], BF16)
+            row_sum = kept.tile([P, CHUNKS], F32)
+            words = e_sb[:].bitcast(F32)
+            for a in range(CHUNKS):
+                nc.scalar.activation(
+                    out=e_sb[:, a * S : (a + 1) * S],
+                    in_=live["att", n][:, a * S : (a + 1) * S],
+                    func=ACT.Exp,
+                    bias=live["neg_max", n][:, a : a + 1],
+                    scale=1.0,
+                    accum_out=row_sum[:, a : a + 1],
+                )
+                if a % 2 == 0:
+                    et = ps_et.tile([P, 512], F32)
+                    live["et", n, a // 2] = et
+                for u in range(2):
+                    first = a * (S // 2) + u * P
+                    nc.tensor.transpose(
+                        et[:, (2 * u + a % 2) * P : (2 * u + a % 2 + 1) * P], words[:, first : first + P], ident_f32[:]
+                    )
+            live["row_sum", n] = row_sum
+
+        def regroup_e(copy, n, pair):
+            if pair == 0:
+                e_grouped = soft.tile([P, 4 * S], BF16, align_bytes=64)
+                live["e_grouped", n] = e_grouped
+            words = live["e_grouped", n][:].bitcast(F32).rearrange("p (c u) -> p c u", u=2)
+            copy(
+                out=words[:, 256 * pair : 256 * (pair + 1), :],
+                in_=live["et", n, pair][:].rearrange("p (u c) -> p c u", u=2),
+            )
+
+        def quantise_e(n):
+            e_codes = kept.tile([P, S], U32, align_bytes=64)
+            e_scales = kept.tile([P, S], U8, align_bytes=64)
+            nc.vector.quantize_mx(out=e_codes[:].bitcast(FP8X4), scales=e_scales[:], in_=live["e_grouped", n][:])
+            live["e_codes", n], live["e_scales", n] = e_codes, e_scales
+
+        def attend(n):
+            o_ps = ps_one.tile([P, CHUNKS * DH], F32)
+            for a in range(CHUNKS):
+                cols = slice(a * P, (a + 1) * P)
+                nc.tensor.matmul_mx(
+                    out=o_ps[:, a * DH : (a + 1) * DH],
+                    lhsT=live["e_codes", n][:, cols].bitcast(FP8X4),
+                    lhsT_scale=live["e_scales", n][:, cols],
+                    rhs=live["v_codes", n][:].bitcast(FP8X4),
+                    rhs_scale=live["v_scales", n][:],
+                    start=True,
+                    stop=True,
+                )
+            live["o_ps", n] = o_ps
+
+        def normalise_and_store(n):
+            b, h = divmod(n, H)
+            if h == 0:
+                o_sb = res.tile([P, CHUNKS * H * DH], F32)
+                live["o_sb", b] = o_sb
+            inv_sum = soft.tile([P, CHUNKS], F32)
+            nc.vector.reciprocal(out=inv_sum[:], in_=live["row_sum", n][:])
+            o_view = live["o_sb", b][:].rearrange("p (a f) -> p a f", a=CHUNKS)
+            nc.vector.tensor_tensor(
+                out=o_view[:, :, h * DH : (h + 1) * DH],
+                in0=live["o_ps", n][:].rearrange("p (a c) -> p a c", a=CHUNKS),
+                in1=inv_sum[:].unsqueeze(2).to_broadcast([P, CHUNKS, DH]),
+                op=ALU.mult,
+            )
+            if h == H - 1:
+                nc.sync.dma_start(out=out[:, b, :].rearrange("(p a) f -> p a f", a=CHUNKS), in_=o_view)
+
+        def is_step(n):
+            return 0 <= n < STEPS
+
+        def is_slot(slot):
+            return -H <= slot < STEPS
+
+        stack.enter_context(tc.manual_schedule())
+        for n in range(-H - X_LEAD - DMA_LEAD, STEPS + V_LAG + 2):
+            if is_slot(n + X_LEAD + DMA_LEAD) and (n + X_LEAD + DMA_LEAD) % H == 0:
+                load_rows((n + X_LEAD + DMA_LEAD) // H)
+            if is_step(n + QK_LEAD + DMA_LEAD) and (n + QK_LEAD + DMA_LEAD) % H == 0:
+                load_qk((n + QK_LEAD + DMA_LEAD) // H)
+            if is_step(n - 2):
+                regroup_e(nc.vector.tensor_copy, n - 2, 1)
+            for a in range(CHUNKS):
+                if is_step(n):
+                    squash(n, a)
+                    add_mask(n, a)
+                if 0 <= n * CHUNKS + a + 2 < STEPS * CHUNKS:
+                    scores(n * CHUNKS + a + 2)
+            if is_slot(n + X_LEAD - 1):
+                regroup_x(n + X_LEAD - 1)
+            if is_step(n - V_LAG - 1):
+                regroup_v(n - V_LAG - 1)
+            if is_step(n - 2):
+                quantise_e(n - 2)
+            if is_slot(n + X_LEAD - 1):
+                quantise_x(n + X_LEAD - 1)
+            if is_step(n - V_LAG - 1):
+                quantise_v(n - V_LAG - 1)
+            if is_step(n - V_LAG - 2):
+                attend(n - V_LAG - 2)
+            if is_step(n - V_LAG):
+                project_v(n - V_LAG)
+            if is_step(n):
+                row_max(n, 0)
+            if is_step(n - 1):
+                exp_and_transpose(n - 1)
+            if is_step(n - V_LAG - 2):
+                normalise_and_store(n - V_LAG - 2)
+            if is_step(n + QK_LEAD - 1):
+                copy_qk(n + QK_LEAD - 1)
+            if is_step(n - 1):
+                regroup_e(nc.scalar.copy, n - 1, 0)
+            if is_step(n):
+                row_max(n, 1)
+            if is_step(n + QK_LEAD):
+                transpose_qk(n + QK_LEAD)
+            if is_slot(n + X_LEAD):
+                transpose_x(n + X_LEAD)

@@ -23,7 +23,7 @@ FLOPS = 2 * S * B * D * H * DH + 2 * 2 * B * H * S * S * DH
 
 QK_LEAD = 3
 X_LEAD = 2
-V_LAG = 4 - X_LEAD
+V_LAG = 5 - X_LEAD
 DMA_LEAD = 4
 
 
@@ -54,38 +54,10 @@ def tile_attention_pa_t_kernel(tc, q, k, x, wv, mask, out):
         nc.vector.tensor_scalar(
             out=mask_term[:], in0=mask_all[:], scalar1=10000.0, scalar2=-10000.0, op0=ALU.mult, op1=ALU.add
         )
-
-        live = {}
-
-        def transpose_piece(rows_sb, piece):
-            g, pair = divmod(piece, 2)
-            words = rows_sb[:].bitcast(F32)
-            xt = ps_one.tile([P, 512], F32)
-            for u in range(2):
-                for s in range(2):
-                    first = (2 * pair + s) * (D // 2) + (2 * g + u) * P
-                    nc.tensor.transpose(
-                        xt[:, (2 * u + s) * P : (2 * u + s + 1) * P], words[:, first : first + P], ident_f32[:]
-                    )
-            return xt
-
-        def regroup_piece(xt, piece, grouped):
-            g, pair = divmod(piece, 2)
-            words = grouped[:].bitcast(F32).rearrange("p (g c u) -> p g c u", g=PASSES, u=2)
-            nc.vector.tensor_copy(
-                out=words[:, g, 256 * pair : 256 * (pair + 1), :], in_=xt[:].rearrange("p (u c) -> p c u", u=2)
-            )
-
-        def quantise_pass(grouped, g, codes, scales):
-            cols = slice(g * S, (g + 1) * S)
-            nc.vector.quantize_mx(
-                out=codes[:, cols].bitcast(FP8X4),
-                scales=scales[:, cols],
-                in_=grouped[:, g * 4 * S : (g + 1) * 4 * S],
-            )
-
         w_codes = const.tile([P, PASSES * S], U32, align_bytes=64)
         w_scales = const.tile([P, PASSES * S], U8, align_bytes=64)
+
+        live = {}
 
         def load_qk(b):
             q_sb = raw.tile([P, H * S], BF16)
@@ -109,24 +81,23 @@ def tile_attention_pa_t_kernel(tc, q, k, x, wv, mask, out):
                     nc.sync.dma_start(out=slabs[:, 2 * u : 2 * u + 2, :], in_=rows[u])
             live["x_sb", b] = x_sb
 
-        def transpose_qk(n):
-            b, h = divmod(n, H)
-            qkt = ps_one.tile([P, 2 * S], BF16)
-            for which, rows_sb in enumerate((live["q_sb", b], live["k_sb", b])):
-                for a in range(CHUNKS):
-                    nc.tensor.transpose(
-                        qkt[:, which * S + a * P : which * S + (a + 1) * P],
-                        rows_sb[:, (h * CHUNKS + a) * DH : (h * CHUNKS + a + 1) * DH],
-                        ident_bf[:],
-                    )
-            live["qkt", n] = qkt
-
-        def transpose_x(slot):
+        def transpose_x(slot, quarter):
             b, h = divmod(slot, H)
-            live["xt", slot] = transpose_piece(live["x_sb", b], h)
+            g, pair = divmod(h, 2)
+            u, s = divmod(quarter, 2)
+            if quarter == 0:
+                xt = ps_one.tile([P, 512], F32)
+                live["xt", slot] = xt
+            first = (2 * pair + s) * (D // 2) + (2 * g + u) * P
+            nc.tensor.transpose(
+                live["xt", slot][:, quarter * P : (quarter + 1) * P],
+                live["x_sb", b][:].bitcast(F32)[:, first : first + P],
+                ident_f32[:],
+            )
 
         def regroup_x(slot):
             b, h = divmod(slot, H)
+            g, pair = divmod(h, 2)
             if h == 0:
                 x_grouped = proj.tile([P, PASSES * 4 * S], BF16, align_bytes=64)
                 live["x_grouped", b] = x_grouped
@@ -136,58 +107,40 @@ def tile_attention_pa_t_kernel(tc, q, k, x, wv, mask, out):
                     x_codes = proj.tile([P, PASSES * S], U32, align_bytes=64)
                     x_scales = proj.tile([P, PASSES * S], U8, align_bytes=64)
                     live["x_codes", b], live["x_scales", b] = x_codes, x_scales
-            regroup_piece(live["xt", slot], h, live["x_grouped", b])
+            words = live["x_grouped", b][:].bitcast(F32).rearrange("p (g c u) -> p g c u", g=PASSES, u=2)
+            nc.vector.tensor_copy(
+                out=words[:, g, 256 * pair : 256 * (pair + 1), :],
+                in_=live["xt", slot][:].rearrange("p (u c) -> p c u", u=2),
+            )
 
         def quantise_x(slot):
             b, h = divmod(slot, H)
-            if h % 2 == 1:
-                quantise_pass(live["x_grouped", b], h // 2, live["x_codes", b], live["x_scales", b])
+            g, pair = divmod(h, 2)
+            if pair == 1:
+                cols = slice(g * S, (g + 1) * S)
+                nc.vector.quantize_mx(
+                    out=live["x_codes", b][:, cols].bitcast(FP8X4),
+                    scales=live["x_scales", b][:, cols],
+                    in_=live["x_grouped", b][:, g * 4 * S : (g + 1) * 4 * S],
+                )
 
-        def copy_qk(n):
-            qk_t = qk_pool.tile([P, 2 * S], BF16)
-            nc.scalar.copy(out=qk_t[:], in_=live["qkt", n][:])
-            live["qk_t", n] = qk_t
-
-        def scores(chunk):
-            n, a = divmod(chunk, CHUNKS)
-            qk_t = live["qk_t", n]
-            s_ps = ps_s.tile([P, S], F32)
-            nc.tensor.matmul(s_ps[:], lhsT=qk_t[:, a * P : (a + 1) * P], rhs=qk_t[:, S : 2 * S], start=True, stop=True)
-            live["s_ps", chunk] = s_ps
-
-        def squash(n, a):
-            if a == 0:
-                att = soft.tile([P, CHUNKS * S], F32)
-                live["att", n] = att
-            nc.scalar.activation(
-                out=live["att", n][:, a * S : (a + 1) * S],
-                in_=live["s_ps", n * CHUNKS + a][:],
-                func=ACT.Tanh,
-                scale=1.0 / math.sqrt(DH),
-            )
-
-        def add_mask(n, a):
-            b = n // H
-            chunk = live["att", n][:, a * S : (a + 1) * S]
-            nc.gpsimd.tensor_tensor(out=chunk, in0=chunk, in1=mask_term[:, b * S : (b + 1) * S], op=ALU.add)
-
-        def project_v(n):
+        def project_v(n, j):
             b, h = divmod(n, H)
-            v_ps = ps_one.tile([P, CHUNKS * DH], F32)
-            for j in range(CHUNKS):
-                for g in range(PASSES):
-                    rows = slice(g * S + j * P, g * S + (j + 1) * P)
-                    cols = slice(g * S + h * DH, g * S + (h + 1) * DH)
-                    nc.tensor.matmul_mx(
-                        out=v_ps[:, j * DH : (j + 1) * DH],
-                        lhsT=live["x_codes", b][:, rows].bitcast(FP8X4),
-                        lhsT_scale=live["x_scales", b][:, rows],
-                        rhs=w_codes[:, cols].bitcast(FP8X4),
-                        rhs_scale=w_scales[:, cols],
-                        start=(g == 0),
-                        stop=(g == PASSES - 1),
-                    )
-            live["v_ps", n] = v_ps
+            if j == 0:
+                v_ps = ps_one.tile([P, CHUNKS * DH], F32)
+                live["v_ps", n] = v_ps
+            for g in range(PASSES):
+                rows = slice(g * S + j * P, g * S + (j + 1) * P)
+                cols = slice(g * S + h * DH, g * S + (h + 1) * DH)
+                nc.tensor.matmul_mx(
+                    out=live["v_ps", n][:, j * DH : (j + 1) * DH],
+                    lhsT=live["x_codes", b][:, rows].bitcast(FP8X4),
+                    lhsT_scale=live["x_scales", b][:, rows],
+                    rhs=w_codes[:, cols].bitcast(FP8X4),
+                    rhs_scale=w_scales[:, cols],
+                    start=(g == 0),
+                    stop=(g == PASSES - 1),
+                )
 
         def regroup_v(n):
             v_grouped = val.tile([P, 4 * DH], BF16, align_bytes=64)
@@ -203,6 +156,45 @@ def tile_attention_pa_t_kernel(tc, q, k, x, wv, mask, out):
             nc.vector.quantize_mx(out=v_codes[:].bitcast(FP8X4), scales=v_scales[:], in_=live["v_grouped", n][:])
             live["v_codes", n], live["v_scales", n] = v_codes, v_scales
 
+        def transpose_qk(n, a):
+            b, h = divmod(n, H)
+            if a == 0:
+                qkt = ps_one.tile([P, 2 * S], BF16)
+                live["qkt", n] = qkt
+            for which, rows_sb in enumerate((live["q_sb", b], live["k_sb", b])):
+                nc.tensor.transpose(
+                    live["qkt", n][:, which * S + a * P : which * S + (a + 1) * P],
+                    rows_sb[:, (h * CHUNKS + a) * DH : (h * CHUNKS + a + 1) * DH],
+                    ident_bf[:],
+                )
+
+        def copy_qk(n):
+            qk_t = qk_pool.tile([P, 2 * S], BF16)
+            nc.scalar.copy(out=qk_t[:], in_=live["qkt", n][:])
+            live["qk_t", n] = qk_t
+
+        def scores(n, a):
+            qk_t = live["qk_t", n]
+            s_ps = ps_s.tile([P, S], F32)
+            nc.tensor.matmul(s_ps[:], lhsT=qk_t[:, a * P : (a + 1) * P], rhs=qk_t[:, S : 2 * S], start=True, stop=True)
+            live["s_ps", n, a] = s_ps
+
+        def squash(n, a):
+            if a == 0:
+                att = soft.tile([P, CHUNKS * S], F32)
+                live["att", n] = att
+            nc.scalar.activation(
+                out=live["att", n][:, a * S : (a + 1) * S],
+                in_=live["s_ps", n, a][:],
+                func=ACT.Tanh,
+                scale=1.0 / math.sqrt(DH),
+            )
+
+        def add_mask(n, a):
+            b = n // H
+            chunk = live["att", n][:, a * S : (a + 1) * S]
+            nc.gpsimd.tensor_tensor(out=chunk, in0=chunk, in1=mask_term[:, b * S : (b + 1) * S], op=ALU.add)
+
         def row_max(n, pair):
             if pair == 0:
                 neg_max = soft.tile([P, CHUNKS], F32)
@@ -213,28 +205,32 @@ def tile_attention_pa_t_kernel(tc, q, k, x, wv, mask, out):
                 out=live["neg_max", n][:, two], in_=att[:, two, :], axis=mybir.AxisListType.X, op=ALU.max, negate=True
             )
 
-        def exp_and_transpose(n):
-            e_sb = soft.tile([P, CHUNKS * S], BF16)
-            row_sum = kept.tile([P, CHUNKS], F32)
-            words = e_sb[:].bitcast(F32)
-            for a in range(CHUNKS):
-                nc.scalar.activation(
-                    out=e_sb[:, a * S : (a + 1) * S],
-                    in_=live["att", n][:, a * S : (a + 1) * S],
-                    func=ACT.Exp,
-                    bias=live["neg_max", n][:, a : a + 1],
-                    scale=1.0,
-                    accum_out=row_sum[:, a : a + 1],
+        def exponential(n, a):
+            if a == 0:
+                e_sb = soft.tile([P, CHUNKS * S], BF16)
+                row_sum = kept.tile([P, CHUNKS], F32)
+                live["e_sb", n], live["row_sum", n] = e_sb, row_sum
+            nc.scalar.activation(
+                out=live["e_sb", n][:, a * S : (a + 1) * S],
+                in_=live["att", n][:, a * S : (a + 1) * S],
+                func=ACT.Exp,
+                bias=live["neg_max", n][:, a : a + 1],
+                scale=1.0,
+                accum_out=live["row_sum", n][:, a : a + 1],
+            )
+
+        def transpose_e(n, a):
+            pair, s = divmod(a, 2)
+            if s == 0:
+                et = ps_et.tile([P, 512], F32)
+                live["et", n, pair] = et
+            for u in range(2):
+                first = a * (S // 2) + u * P
+                nc.tensor.transpose(
+                    live["et", n, pair][:, (2 * u + s) * P : (2 * u + s + 1) * P],
+                    live["e_sb", n][:].bitcast(F32)[:, first : first + P],
+                    ident_f32[:],
                 )
-                if a % 2 == 0:
-                    et = ps_et.tile([P, 512], F32)
-                    live["et", n, a // 2] = et
-                for u in range(2):
-                    first = a * (S // 2) + u * P
-                    nc.tensor.transpose(
-                        et[:, (2 * u + a % 2) * P : (2 * u + a % 2 + 1) * P], words[:, first : first + P], ident_f32[:]
-                    )
-            live["row_sum", n] = row_sum
 
         def regroup_e(copy, n, pair):
             if pair == 0:
@@ -252,20 +248,20 @@ def tile_attention_pa_t_kernel(tc, q, k, x, wv, mask, out):
             nc.vector.quantize_mx(out=e_codes[:].bitcast(FP8X4), scales=e_scales[:], in_=live["e_grouped", n][:])
             live["e_codes", n], live["e_scales", n] = e_codes, e_scales
 
-        def attend(n):
-            o_ps = ps_one.tile([P, CHUNKS * DH], F32)
-            for a in range(CHUNKS):
-                cols = slice(a * P, (a + 1) * P)
-                nc.tensor.matmul_mx(
-                    out=o_ps[:, a * DH : (a + 1) * DH],
-                    lhsT=live["e_codes", n][:, cols].bitcast(FP8X4),
-                    lhsT_scale=live["e_scales", n][:, cols],
-                    rhs=live["v_codes", n][:].bitcast(FP8X4),
-                    rhs_scale=live["v_scales", n][:],
-                    start=True,
-                    stop=True,
-                )
-            live["o_ps", n] = o_ps
+        def attend(n, a):
+            if a == 0:
+                o_ps = ps_one.tile([P, CHUNKS * DH], F32)
+                live["o_ps", n] = o_ps
+            cols = slice(a * P, (a + 1) * P)
+            nc.tensor.matmul_mx(
+                out=live["o_ps", n][:, a * DH : (a + 1) * DH],
+                lhsT=live["e_codes", n][:, cols].bitcast(FP8X4),
+                lhsT_scale=live["e_scales", n][:, cols],
+                rhs=live["v_codes", n][:].bitcast(FP8X4),
+                rhs_scale=live["v_scales", n][:],
+                start=True,
+                stop=True,
+            )
 
         def normalise_and_store(n):
             b, h = divmod(n, H)
@@ -296,41 +292,43 @@ def tile_attention_pa_t_kernel(tc, q, k, x, wv, mask, out):
                 load_rows((n + X_LEAD + DMA_LEAD) // H)
             if is_step(n + QK_LEAD + DMA_LEAD) and (n + QK_LEAD + DMA_LEAD) % H == 0:
                 load_qk((n + QK_LEAD + DMA_LEAD) // H)
-            if is_step(n - 2):
-                regroup_e(nc.vector.tensor_copy, n - 2, 1)
-            for a in range(CHUNKS):
-                if is_step(n):
-                    squash(n, a)
-                    add_mask(n, a)
-                if 0 <= n * CHUNKS + a + 2 < STEPS * CHUNKS:
-                    scores(n * CHUNKS + a + 2)
+            if is_step(n + QK_LEAD - 1):
+                copy_qk(n + QK_LEAD - 1)
             if is_slot(n + X_LEAD - 1):
                 regroup_x(n + X_LEAD - 1)
             if is_step(n - V_LAG - 1):
                 regroup_v(n - V_LAG - 1)
+            if is_step(n - 2):
+                regroup_e(nc.vector.tensor_copy, n - 2, 1)
+            if is_step(n - 1):
+                row_max(n - 1, 1)
+            for a in range(CHUNKS):
+                if is_step(n):
+                    squash(n, a)
+                    add_mask(n, a)
+                ahead_n, ahead_a = divmod(n * CHUNKS + a + 2, CHUNKS)
+                if is_step(ahead_n):
+                    scores(ahead_n, ahead_a)
+                if is_step(n - V_LAG - 2):
+                    attend(n - V_LAG - 2, a)
+                if is_step(n - V_LAG):
+                    project_v(n - V_LAG, a)
+                if is_step(n + QK_LEAD):
+                    transpose_qk(n + QK_LEAD, a)
+                if is_slot(n + X_LEAD):
+                    transpose_x(n + X_LEAD, a)
+                if is_step(n - 1):
+                    exponential(n - 1, a)
+                    transpose_e(n - 1, a)
+            if is_step(n - 1):
+                regroup_e(nc.scalar.copy, n - 1, 0)
             if is_step(n - 2):
                 quantise_e(n - 2)
             if is_slot(n + X_LEAD - 1):
                 quantise_x(n + X_LEAD - 1)
             if is_step(n - V_LAG - 1):
                 quantise_v(n - V_LAG - 1)
-            if is_step(n - V_LAG - 2):
-                attend(n - V_LAG - 2)
-            if is_step(n - V_LAG):
-                project_v(n - V_LAG)
             if is_step(n):
                 row_max(n, 0)
-            if is_step(n - 1):
-                exp_and_transpose(n - 1)
             if is_step(n - V_LAG - 2):
                 normalise_and_store(n - V_LAG - 2)
-            if is_step(n + QK_LEAD - 1):
-                copy_qk(n + QK_LEAD - 1)
-            if is_step(n - 1):
-                regroup_e(nc.scalar.copy, n - 1, 0)
-            if is_step(n):
-                row_max(n, 1)
-            if is_step(n + QK_LEAD):
-                transpose_qk(n + QK_LEAD)
-            if is_slot(n + X_LEAD):
-                transpose_x(n + X_LEAD)

@@ -21,7 +21,7 @@ STEPS = B * H
 
 FLOPS = 2 * S * B * D * H * DH + 2 * 2 * B * H * S * S * DH
 
-QK_LEAD = 3
+QK_LEAD = 2
 X_LEAD = 2
 V_LAG = 5 - X_LEAD
 DMA_LEAD = 4
@@ -39,21 +39,15 @@ def tile_attention_pa_t_kernel(tc, q, k, x, wv, mask, out):
         soft = pool("soft", 3)
         kept = pool("kept", V_LAG + 4)
         val = pool("val", 3)
-        res = pool("res", 2)
+        res = pool("res", 3)
         ps_s = psum("ps_s", 2)
         ps_et = psum("ps_et", 2)
-        ps_one = psum("ps_one", 1)
+        ps_two = psum("ps_two", 2)
 
         ident_f32 = const.tile([P, P], F32)
         make_identity(nc, ident_f32[:])
         ident_bf = const.tile([P, P], BF16)
         make_identity(nc, ident_bf[:])
-        mask_all = const.tile([P, B * S], BF16)
-        nc.scalar.dma_start(out=mask_all[:], in_=mask.rearrange("b t -> (b t)").partition_broadcast(P))
-        mask_term = const.tile([P, B * S], F32)
-        nc.vector.tensor_scalar(
-            out=mask_term[:], in0=mask_all[:], scalar1=10000.0, scalar2=-10000.0, op0=ALU.mult, op1=ALU.add
-        )
         w_codes = const.tile([P, PASSES * S], U32, align_bytes=64)
         w_scales = const.tile([P, PASSES * S], U8, align_bytes=64)
 
@@ -68,7 +62,16 @@ def tile_attention_pa_t_kernel(tc, q, k, x, wv, mask, out):
             nc.sync.dma_start(
                 out=k_sb[:].rearrange("p (f c) -> p f c", c=DH), in_=k[b].rearrange("h (a p) c -> p (h a) c", p=P)
             )
-            live["q_sb", b], live["k_sb", b] = q_sb, k_sb
+            mask_sb = raw.tile([P, S], BF16)
+            nc.sync.dma_start(out=mask_sb[:], in_=mask[b].partition_broadcast(P))
+            live["q_sb", b], live["k_sb", b], live["mask_sb", b] = q_sb, k_sb, mask_sb
+
+        def make_mask_term(b):
+            mask_term = raw.tile([P, S], F32)
+            nc.vector.tensor_scalar(
+                out=mask_term[:], in0=live["mask_sb", b][:], scalar1=10000.0, scalar2=-10000.0, op0=ALU.mult, op1=ALU.add
+            )
+            live["mask_term", b] = mask_term
 
         def load_rows(b):
             x_sb = raw.tile([P, CHUNKS * D], BF16)
@@ -86,7 +89,7 @@ def tile_attention_pa_t_kernel(tc, q, k, x, wv, mask, out):
             g, pair = divmod(h, 2)
             u, s = divmod(quarter, 2)
             if quarter == 0:
-                xt = ps_one.tile([P, 512], F32)
+                xt = ps_two.tile([P, 512], F32, tag="x_or_v")
                 live["xt", slot] = xt
             first = (2 * pair + s) * (D // 2) + (2 * g + u) * P
             nc.tensor.transpose(
@@ -127,7 +130,7 @@ def tile_attention_pa_t_kernel(tc, q, k, x, wv, mask, out):
         def project_v(n, j):
             b, h = divmod(n, H)
             if j == 0:
-                v_ps = ps_one.tile([P, CHUNKS * DH], F32)
+                v_ps = ps_two.tile([P, CHUNKS * DH], F32, tag="x_or_v")
                 live["v_ps", n] = v_ps
             for g in range(PASSES):
                 rows = slice(g * S + j * P, g * S + (j + 1) * P)
@@ -159,7 +162,7 @@ def tile_attention_pa_t_kernel(tc, q, k, x, wv, mask, out):
         def transpose_qk(n, a):
             b, h = divmod(n, H)
             if a == 0:
-                qkt = ps_one.tile([P, 2 * S], BF16)
+                qkt = ps_two.tile([P, 2 * S], BF16, tag="qk_or_o")
                 live["qkt", n] = qkt
             for which, rows_sb in enumerate((live["q_sb", b], live["k_sb", b])):
                 nc.tensor.transpose(
@@ -170,7 +173,7 @@ def tile_attention_pa_t_kernel(tc, q, k, x, wv, mask, out):
 
         def copy_qk(n):
             qk_t = qk_pool.tile([P, 2 * S], BF16)
-            nc.scalar.copy(out=qk_t[:], in_=live["qkt", n][:])
+            nc.vector.tensor_copy(out=qk_t[:], in_=live["qkt", n][:])
             live["qk_t", n] = qk_t
 
         def scores(n, a):
@@ -193,7 +196,7 @@ def tile_attention_pa_t_kernel(tc, q, k, x, wv, mask, out):
         def add_mask(n, a):
             b = n // H
             chunk = live["att", n][:, a * S : (a + 1) * S]
-            nc.gpsimd.tensor_tensor(out=chunk, in0=chunk, in1=mask_term[:, b * S : (b + 1) * S], op=ALU.add)
+            nc.gpsimd.tensor_tensor(out=chunk, in0=chunk, in1=live["mask_term", b][:], op=ALU.add)
 
         def row_max(n, pair):
             if pair == 0:
@@ -250,7 +253,7 @@ def tile_attention_pa_t_kernel(tc, q, k, x, wv, mask, out):
 
         def attend(n, a):
             if a == 0:
-                o_ps = ps_one.tile([P, CHUNKS * DH], F32)
+                o_ps = ps_two.tile([P, CHUNKS * DH], F32, tag="qk_or_o")
                 live["o_ps", n] = o_ps
             cols = slice(a * P, (a + 1) * P)
             nc.tensor.matmul_mx(
@@ -263,22 +266,24 @@ def tile_attention_pa_t_kernel(tc, q, k, x, wv, mask, out):
                 stop=True,
             )
 
+        def invert_row_sum(n):
+            inv_sum = kept.tile([P, CHUNKS], F32)
+            nc.vector.reciprocal(out=inv_sum[:], in_=live["row_sum", n][:])
+            live["inv_sum", n] = inv_sum
+
         def normalise_and_store(n):
             b, h = divmod(n, H)
-            if h == 0:
-                o_sb = res.tile([P, CHUNKS * H * DH], F32)
-                live["o_sb", b] = o_sb
-            inv_sum = soft.tile([P, CHUNKS], F32)
-            nc.vector.reciprocal(out=inv_sum[:], in_=live["row_sum", n][:])
-            o_view = live["o_sb", b][:].rearrange("p (a f) -> p a f", a=CHUNKS)
+            o_sb = res.tile([P, CHUNKS * DH], F32)
+            o_view = o_sb[:].rearrange("p (a c) -> p a c", a=CHUNKS)
             nc.vector.tensor_tensor(
-                out=o_view[:, :, h * DH : (h + 1) * DH],
+                out=o_view,
                 in0=live["o_ps", n][:].rearrange("p (a c) -> p a c", a=CHUNKS),
-                in1=inv_sum[:].unsqueeze(2).to_broadcast([P, CHUNKS, DH]),
+                in1=live["inv_sum", n][:].unsqueeze(2).to_broadcast([P, CHUNKS, DH]),
                 op=ALU.mult,
             )
-            if h == H - 1:
-                nc.sync.dma_start(out=out[:, b, :].rearrange("(p a) f -> p a f", a=CHUNKS), in_=o_view)
+            nc.sync.dma_start(
+                out=out[:, b, h * DH : (h + 1) * DH].rearrange("(p a) c -> p a c", a=CHUNKS), in_=o_view
+            )
 
         def is_step(n):
             return 0 <= n < STEPS
@@ -288,12 +293,14 @@ def tile_attention_pa_t_kernel(tc, q, k, x, wv, mask, out):
 
         stack.enter_context(tc.manual_schedule())
         for n in range(-H - X_LEAD - DMA_LEAD, STEPS + V_LAG + 2):
-            if is_slot(n + X_LEAD + DMA_LEAD) and (n + X_LEAD + DMA_LEAD) % H == 0:
-                load_rows((n + X_LEAD + DMA_LEAD) // H)
             if is_step(n + QK_LEAD + DMA_LEAD) and (n + QK_LEAD + DMA_LEAD) % H == 0:
                 load_qk((n + QK_LEAD + DMA_LEAD) // H)
+            if is_slot(n + X_LEAD + DMA_LEAD) and (n + X_LEAD + DMA_LEAD) % H == 0:
+                load_rows((n + X_LEAD + DMA_LEAD) // H)
             if is_step(n + QK_LEAD - 1):
                 copy_qk(n + QK_LEAD - 1)
+            if is_step(n + 1) and (n + 1) % H == 0:
+                make_mask_term((n + 1) // H)
             if is_slot(n + X_LEAD - 1):
                 regroup_x(n + X_LEAD - 1)
             if is_step(n - V_LAG - 1):
@@ -302,6 +309,8 @@ def tile_attention_pa_t_kernel(tc, q, k, x, wv, mask, out):
                 regroup_e(nc.vector.tensor_copy, n - 2, 1)
             if is_step(n - 1):
                 row_max(n - 1, 1)
+            if is_step(n - V_LAG - 2):
+                invert_row_sum(n - V_LAG - 2)
             for a in range(CHUNKS):
                 if is_step(n):
                     squash(n, a)

@@ -25,6 +25,7 @@ QK_LEAD = 2
 X_LEAD = 2
 V_LAG = 5 - X_LEAD
 DMA_LEAD = 4
+VECTOR_MASK_CHUNK = 1
 
 
 def tile_attention_pa_t_kernel(tc, q, k, x, wv, mask, out):
@@ -173,7 +174,7 @@ def tile_attention_pa_t_kernel(tc, q, k, x, wv, mask, out):
 
         def copy_qk(n):
             qk_t = qk_pool.tile([P, 2 * S], BF16)
-            nc.vector.tensor_copy(out=qk_t[:], in_=live["qkt", n][:])
+            nc.scalar.copy(out=qk_t[:], in_=live["qkt", n][:])
             live["qk_t", n] = qk_t
 
         def scores(n, a):
@@ -193,10 +194,10 @@ def tile_attention_pa_t_kernel(tc, q, k, x, wv, mask, out):
                 scale=1.0 / math.sqrt(DH),
             )
 
-        def add_mask(n, a):
+        def add_mask(engine, n, a):
             b = n // H
             chunk = live["att", n][:, a * S : (a + 1) * S]
-            nc.gpsimd.tensor_tensor(out=chunk, in0=chunk, in1=live["mask_term", b][:], op=ALU.add)
+            engine.tensor_tensor(out=chunk, in0=chunk, in1=live["mask_term", b][:], op=ALU.add)
 
         def row_max(n, pair):
             if pair == 0:
@@ -314,7 +315,8 @@ def tile_attention_pa_t_kernel(tc, q, k, x, wv, mask, out):
             for a in range(CHUNKS):
                 if is_step(n):
                     squash(n, a)
-                    add_mask(n, a)
+                    if a != VECTOR_MASK_CHUNK:
+                        add_mask(nc.gpsimd, n, a)
                 ahead_n, ahead_a = divmod(n * CHUNKS + a + 2, CHUNKS)
                 if is_step(ahead_n):
                     scores(ahead_n, ahead_a)
@@ -331,6 +333,8 @@ def tile_attention_pa_t_kernel(tc, q, k, x, wv, mask, out):
                     transpose_e(n - 1, a)
             if is_step(n - 1):
                 regroup_e(nc.scalar.copy, n - 1, 0)
+            if is_step(n):
+                add_mask(nc.vector, n, VECTOR_MASK_CHUNK)
             if is_step(n - 2):
                 quantise_e(n - 2)
             if is_slot(n + X_LEAD - 1):

@@ -23,9 +23,8 @@ FLOPS = 2 * S * B * D * H * DH + 2 * 2 * B * H * S * S * DH
 
 QK_LEAD = 2
 X_LEAD = 2
-V_LAG = 5 - X_LEAD
+V_LAG = 2
 DMA_LEAD = 4
-VECTOR_MASK_CHUNK = 1
 
 
 def tile_attention_pa_t_kernel(tc, q, k, x, wv, mask, out):
@@ -36,9 +35,9 @@ def tile_attention_pa_t_kernel(tc, q, k, x, wv, mask, out):
         const = pool("const", 1)
         raw = pool("raw", 2)
         proj = pool("proj", 2)
-        qk_pool = pool("qk", QK_LEAD + 1)
+        qk_pool = pool("qk", QK_LEAD + 2)
         soft = pool("soft", 3)
-        kept = pool("kept", V_LAG + 4)
+        kept = pool("kept", 6)
         val = pool("val", 3)
         res = pool("res", 3)
         ps_s = psum("ps_s", 2)
@@ -293,55 +292,58 @@ def tile_attention_pa_t_kernel(tc, q, k, x, wv, mask, out):
             return -H <= slot < STEPS
 
         stack.enter_context(tc.manual_schedule())
-        for n in range(-H - X_LEAD - DMA_LEAD, STEPS + V_LAG + 2):
+        E = 2
+        AT = 4
+        for n in range(-H - X_LEAD - DMA_LEAD, STEPS + AT + 2):
             if is_step(n + QK_LEAD + DMA_LEAD) and (n + QK_LEAD + DMA_LEAD) % H == 0:
                 load_qk((n + QK_LEAD + DMA_LEAD) // H)
             if is_slot(n + X_LEAD + DMA_LEAD) and (n + X_LEAD + DMA_LEAD) % H == 0:
                 load_rows((n + X_LEAD + DMA_LEAD) // H)
-            if is_step(n + QK_LEAD - 1):
-                copy_qk(n + QK_LEAD - 1)
-            if is_step(n + 1) and (n + 1) % H == 0:
-                make_mask_term((n + 1) // H)
-            if is_slot(n + X_LEAD - 1):
-                regroup_x(n + X_LEAD - 1)
-            if is_step(n - V_LAG - 1):
-                regroup_v(n - V_LAG - 1)
-            if is_step(n - 2):
-                regroup_e(nc.vector.tensor_copy, n - 2, 1)
-            if is_step(n - 1):
-                row_max(n - 1, 1)
-            if is_step(n - V_LAG - 2):
-                invert_row_sum(n - V_LAG - 2)
+
             for a in range(CHUNKS):
                 if is_step(n):
                     squash(n, a)
-                    if a != VECTOR_MASK_CHUNK:
-                        add_mask(nc.gpsimd, n, a)
+                    add_mask(nc.gpsimd, n, a)
                 ahead_n, ahead_a = divmod(n * CHUNKS + a + 2, CHUNKS)
                 if is_step(ahead_n):
                     scores(ahead_n, ahead_a)
-                if is_step(n - V_LAG - 2):
-                    attend(n - V_LAG - 2, a)
-                if is_step(n - V_LAG):
-                    project_v(n - V_LAG, a)
-                if is_step(n + QK_LEAD):
-                    transpose_qk(n + QK_LEAD, a)
-                if is_slot(n + X_LEAD):
-                    transpose_x(n + X_LEAD, a)
-                if is_step(n - 1):
-                    exponential(n - 1, a)
-                    transpose_e(n - 1, a)
+                if a == 3 and is_step(n - AT):
+                    for j in range(4):
+                        attend(n - AT, j)
+                if a == 1 and is_step(n - V_LAG):
+                    for j in range(4):
+                        project_v(n - V_LAG, j)
+                if a == 0 and is_step(n + QK_LEAD):
+                    for j in range(4):
+                        transpose_qk(n + QK_LEAD, j)
+                if a == 2 and is_slot(n + X_LEAD):
+                    for j in range(4):
+                        transpose_x(n + X_LEAD, j)
+                if is_step(n - E):
+                    exponential(n - E, a)
+                    transpose_e(n - E, a)
+                if a == 2 and is_step(n + QK_LEAD):
+                    copy_qk(n + QK_LEAD)
+            if is_step(n - E):
+                regroup_e(nc.scalar.copy, n - E, 0)
+            if is_step(n + 1) and (n + 1) % H == 0:
+                make_mask_term((n + 1) // H)
+            if is_step(n - E - 1):
+                regroup_e(nc.vector.tensor_copy, n - E - 1, 1)
+            if is_step(n - AT - 1):
+                invert_row_sum(n - AT - 1)
+                normalise_and_store(n - AT - 1)
             if is_step(n - 1):
-                regroup_e(nc.scalar.copy, n - 1, 0)
-            if is_step(n):
-                add_mask(nc.vector, n, VECTOR_MASK_CHUNK)
-            if is_step(n - 2):
-                quantise_e(n - 2)
-            if is_slot(n + X_LEAD - 1):
-                quantise_x(n + X_LEAD - 1)
-            if is_step(n - V_LAG - 1):
-                quantise_v(n - V_LAG - 1)
-            if is_step(n):
-                row_max(n, 0)
-            if is_step(n - V_LAG - 2):
-                normalise_and_store(n - V_LAG - 2)
+                row_max(n - 1, 0)
+            if is_step(n - V_LAG):
+                regroup_v(n - V_LAG)
+            if is_step(n - 1):
+                row_max(n - 1, 1)
+            if is_slot(n + X_LEAD):
+                regroup_x(n + X_LEAD)
+            if is_step(n - E - 1):
+                quantise_e(n - E - 1)
+            if is_slot(n + X_LEAD):
+                quantise_x(n + X_LEAD)
+            if is_step(n - V_LAG):
+                quantise_v(n - V_LAG)

@@ -24,6 +24,8 @@ FLOPS = 2 * S * B * D * H * DH + 2 * 2 * B * H * S * S * DH
 QK_LEAD = 2
 X_LEAD = 2
 V_LAG = 2
+EXP_LAG = 2
+ATTEND_LAG = 4
 DMA_LEAD = 4
 
 
@@ -37,7 +39,7 @@ def tile_attention_pa_t_kernel(tc, q, k, x, wv, mask, out):
         proj = pool("proj", 2)
         qk_pool = pool("qk", QK_LEAD + 2)
         soft = pool("soft", 3)
-        kept = pool("kept", 6)
+        kept = pool("kept", 8)
         val = pool("val", 3)
         res = pool("res", 3)
         ps_s = psum("ps_s", 2)
@@ -98,7 +100,7 @@ def tile_attention_pa_t_kernel(tc, q, k, x, wv, mask, out):
                 ident_f32[:],
             )
 
-        def regroup_x(slot):
+        def regroup_x(copy, slot):
             b, h = divmod(slot, H)
             g, pair = divmod(h, 2)
             if h == 0:
@@ -111,7 +113,7 @@ def tile_attention_pa_t_kernel(tc, q, k, x, wv, mask, out):
                     x_scales = proj.tile([P, PASSES * S], U8, align_bytes=64)
                     live["x_codes", b], live["x_scales", b] = x_codes, x_scales
             words = live["x_grouped", b][:].bitcast(F32).rearrange("p (g c u) -> p g c u", g=PASSES, u=2)
-            nc.vector.tensor_copy(
+            copy(
                 out=words[:, g, 256 * pair : 256 * (pair + 1), :],
                 in_=live["xt", slot][:].rearrange("p (u c) -> p c u", u=2),
             )
@@ -193,10 +195,12 @@ def tile_attention_pa_t_kernel(tc, q, k, x, wv, mask, out):
                 scale=1.0 / math.sqrt(DH),
             )
 
-        def add_mask(engine, n, a):
+        def add_mask_two(n, pair):
             b = n // H
-            chunk = live["att", n][:, a * S : (a + 1) * S]
-            engine.tensor_tensor(out=chunk, in0=chunk, in1=live["mask_term", b][:], op=ALU.add)
+            two = live["att", n][:, pair * 2 * S : (pair + 1) * 2 * S].rearrange("p (a t) -> p a t", a=2)
+            nc.gpsimd.tensor_tensor(
+                out=two, in0=two, in1=live["mask_term", b][:].unsqueeze(1).to_broadcast([P, 2, S]), op=ALU.add
+            )
 
         def row_max(n, pair):
             if pair == 0:
@@ -288,62 +292,68 @@ def tile_attention_pa_t_kernel(tc, q, k, x, wv, mask, out):
         def is_step(n):
             return 0 <= n < STEPS
 
-        def is_slot(slot):
-            return -H <= slot < STEPS
+        def slots(n):
+            return [s for s in (n + X_LEAD,) if -H <= s < STEPS]
+
+        def projects(n):
+            return [m for m in (n - V_LAG,) if is_step(m)]
 
         stack.enter_context(tc.manual_schedule())
-        E = 2
-        AT = 4
-        for n in range(-H - X_LEAD - DMA_LEAD, STEPS + AT + 2):
+        for n in range(-H - X_LEAD - DMA_LEAD, STEPS + ATTEND_LAG + 2):
             if is_step(n + QK_LEAD + DMA_LEAD) and (n + QK_LEAD + DMA_LEAD) % H == 0:
                 load_qk((n + QK_LEAD + DMA_LEAD) // H)
-            if is_slot(n + X_LEAD + DMA_LEAD) and (n + X_LEAD + DMA_LEAD) % H == 0:
+            if -H <= n + X_LEAD + DMA_LEAD < STEPS and (n + X_LEAD + DMA_LEAD) % H == 0:
                 load_rows((n + X_LEAD + DMA_LEAD) // H)
-
             for a in range(CHUNKS):
                 if is_step(n):
                     squash(n, a)
-                    add_mask(nc.gpsimd, n, a)
+                    if a % 2 == 1:
+                        add_mask_two(n, a // 2)
                 ahead_n, ahead_a = divmod(n * CHUNKS + a + 2, CHUNKS)
                 if is_step(ahead_n):
                     scores(ahead_n, ahead_a)
-                if a == 3 and is_step(n - AT):
-                    for j in range(4):
-                        attend(n - AT, j)
-                if a == 1 and is_step(n - V_LAG):
-                    for j in range(4):
-                        project_v(n - V_LAG, j)
+                if a == 3 and is_step(n - ATTEND_LAG):
+                    for j in range(CHUNKS):
+                        attend(n - ATTEND_LAG, j)
+                if a == 1:
+                    for m in projects(n):
+                        for j in range(CHUNKS):
+                            project_v(m, j)
                 if a == 0 and is_step(n + QK_LEAD):
-                    for j in range(4):
+                    for j in range(CHUNKS):
                         transpose_qk(n + QK_LEAD, j)
-                if a == 2 and is_slot(n + X_LEAD):
-                    for j in range(4):
-                        transpose_x(n + X_LEAD, j)
-                if is_step(n - E):
-                    exponential(n - E, a)
-                    transpose_e(n - E, a)
+                if a == 2:
+                    for slot in slots(n):
+                        for j in range(CHUNKS):
+                            transpose_x(slot, j)
+                if a == 3 and is_step(n + 1) and (n + 1) % H == 0:
+                    make_mask_term((n + 1) // H)
+
+                if is_step(n - EXP_LAG):
+                    exponential(n - EXP_LAG, a)
+                    transpose_e(n - EXP_LAG, a)
                 if a == 2 and is_step(n + QK_LEAD):
                     copy_qk(n + QK_LEAD)
-            if is_step(n - E):
-                regroup_e(nc.scalar.copy, n - E, 0)
-            if is_step(n + 1) and (n + 1) % H == 0:
-                make_mask_term((n + 1) // H)
-            if is_step(n - E - 1):
-                regroup_e(nc.vector.tensor_copy, n - E - 1, 1)
-            if is_step(n - AT - 1):
-                invert_row_sum(n - AT - 1)
-                normalise_and_store(n - AT - 1)
+            if is_step(n - EXP_LAG):
+                regroup_e(nc.scalar.copy, n - EXP_LAG, 0)
+            if is_step(n - EXP_LAG) and (False):
+                regroup_e(nc.scalar.copy, n - EXP_LAG, 1)
+            if is_step(n - EXP_LAG - 1):
+                regroup_e(nc.vector.tensor_copy, n - EXP_LAG - 1, 1)
+            if is_step(n - ATTEND_LAG - 1):
+                invert_row_sum(n - ATTEND_LAG - 1)
+                normalise_and_store(n - ATTEND_LAG - 1)
             if is_step(n - 1):
                 row_max(n - 1, 0)
-            if is_step(n - V_LAG):
-                regroup_v(n - V_LAG)
+            for m in projects(n):
+                regroup_v(m)
             if is_step(n - 1):
                 row_max(n - 1, 1)
-            if is_slot(n + X_LEAD):
-                regroup_x(n + X_LEAD)
-            if is_step(n - E - 1):
-                quantise_e(n - E - 1)
-            if is_slot(n + X_LEAD):
-                quantise_x(n + X_LEAD)
-            if is_step(n - V_LAG):
-                quantise_v(n - V_LAG)
+            for slot in slots(n):
+                regroup_x(nc.vector.tensor_copy, slot)
+            if is_step(n - EXP_LAG - 1):
+                quantise_e(n - EXP_LAG - 1)
+            for slot in slots(n):
+                quantise_x(slot)
+            for m in projects(n):
+                quantise_v(m)

@@ -21,7 +21,6 @@ STEPS = B * H
 
 FLOPS = 2 * S * B * D * H * DH + 2 * 2 * B * H * S * S * DH
 
-QK_LEAD = 2
 X_LEAD = 2
 V_LAG = 2
 EXP_LAG = 2
@@ -37,10 +36,10 @@ def tile_attention_pa_t_kernel(tc, q, k, x, wv, mask, out):
         const = pool("const", 1)
         raw = pool("raw", 2)
         proj = pool("proj", 2)
-        qk_pool = pool("qk", QK_LEAD + 2)
+        qk_pool = pool("qk", 4)
         soft = pool("soft", 3)
-        kept = pool("kept", 8)
-        val = pool("val", 3)
+        kept = pool("kept", 10)
+        val = pool("val", 4)
         res = pool("res", 3)
         ps_s = psum("ps_s", 2)
         ps_et = psum("ps_et", 2)
@@ -57,13 +56,16 @@ def tile_attention_pa_t_kernel(tc, q, k, x, wv, mask, out):
 
         def load_qk(b):
             q_sb = raw.tile([P, H * S], BF16)
-            nc.sync.dma_start(
-                out=q_sb[:].rearrange("p (h f) -> p h f", h=H), in_=q[b].rearrange("h (p a) c -> p h (a c)", a=CHUNKS)
-            )
             k_sb = raw.tile([P, H * S], BF16)
-            nc.sync.dma_start(
-                out=k_sb[:].rearrange("p (f c) -> p f c", c=DH), in_=k[b].rearrange("h (a p) c -> p (h a) c", p=P)
-            )
+            for lo, hi in ((0, 1), (1, H)):
+                nc.sync.dma_start(
+                    out=q_sb[:, lo * S : hi * S].rearrange("p (h f) -> p h f", f=S),
+                    in_=q[b, lo:hi].rearrange("h (p a) c -> p h (a c)", a=CHUNKS),
+                )
+                nc.sync.dma_start(
+                    out=k_sb[:, lo * S : hi * S].rearrange("p (f c) -> p f c", c=DH),
+                    in_=k[b, lo:hi].rearrange("h (a p) c -> p (h a) c", p=P),
+                )
             mask_sb = raw.tile([P, S], BF16)
             nc.sync.dma_start(out=mask_sb[:], in_=mask[b].partition_broadcast(P))
             live["q_sb", b], live["k_sb", b], live["mask_sb", b] = q_sb, k_sb, mask_sb
@@ -147,9 +149,9 @@ def tile_attention_pa_t_kernel(tc, q, k, x, wv, mask, out):
                     stop=(g == PASSES - 1),
                 )
 
-        def regroup_v(n):
+        def regroup_v(copy, n):
             v_grouped = val.tile([P, 4 * DH], BF16, align_bytes=64)
-            nc.vector.tensor_copy(
+            copy(
                 out=v_grouped[:].rearrange("p (c j) -> p c j", j=4),
                 in_=live["v_ps", n][:].rearrange("p (j c) -> p c j", j=4),
             )
@@ -195,22 +197,21 @@ def tile_attention_pa_t_kernel(tc, q, k, x, wv, mask, out):
                 scale=1.0 / math.sqrt(DH),
             )
 
-        def add_mask_two(n, pair):
-            b = n // H
-            two = live["att", n][:, pair * 2 * S : (pair + 1) * 2 * S].rearrange("p (a t) -> p a t", a=2)
-            nc.gpsimd.tensor_tensor(
-                out=two, in0=two, in1=live["mask_term", b][:].unsqueeze(1).to_broadcast([P, 2, S]), op=ALU.add
-            )
+        def add_mask(engine, n, lo, hi):
+            chunks = live["att", n][:, lo * S : hi * S].rearrange("p (a t) -> p a t", a=hi - lo)
+            term = live["mask_term", n // H][:].unsqueeze(1).to_broadcast([P, hi - lo, S])
+            engine.tensor_tensor(out=chunks, in0=chunks, in1=term, op=ALU.add)
 
-        def row_max(n, pair):
-            if pair == 0:
-                neg_max = soft.tile([P, CHUNKS], F32)
-                live["neg_max", n] = neg_max
-            att = live["att", n][:].rearrange("p (a t) -> p a t", a=CHUNKS)
-            two = slice(2 * pair, 2 * pair + 2)
+        def row_max(n):
+            neg_max = soft.tile([P, CHUNKS], F32)
             nc.vector.tensor_reduce(
-                out=live["neg_max", n][:, two], in_=att[:, two, :], axis=mybir.AxisListType.X, op=ALU.max, negate=True
+                out=neg_max[:],
+                in_=live["att", n][:].rearrange("p (a t) -> p a t", a=CHUNKS),
+                axis=mybir.AxisListType.X,
+                op=ALU.max,
+                negate=True,
             )
+            live["neg_max", n] = neg_max
 
         def exponential(n, a):
             if a == 0:
@@ -292,65 +293,101 @@ def tile_attention_pa_t_kernel(tc, q, k, x, wv, mask, out):
         def is_step(n):
             return 0 <= n < STEPS
 
+        head_slots = {1: (-4, -3, -2, -1), 2: (0, 1, 2, 3), 3: (4,), 4: (5,)}
+        head_projects = {3: (0, 1), 4: (2,), 5: (3,)}
+
         def slots(n):
-            return [s for s in (n + X_LEAD,) if -H <= s < STEPS]
+            return list(head_slots.get(n, ())) + [s for s in (n + X_LEAD,) if 6 <= s < STEPS]
 
         def projects(n):
-            return [m for m in (n - V_LAG,) if is_step(m)]
+            return list(head_projects.get(n, ())) + [m for m in (n - V_LAG,) if 4 <= m < STEPS]
+
+        def attends(n):
+            return [m for m in (n - ATTEND_LAG,) if is_step(m)]
+
+        def mask_plan(n):
+            return [("v" if n == 0 else "g", lo, lo + 2) for lo in (0, 2)]
+
+        def scalar_takes_e1(n):
+            return STEPS - EXP_LAG <= n < STEPS - 1
+
+        def prepare_qk(n):
+            for j in range(CHUNKS):
+                transpose_qk(n, j)
+            copy_qk(n)
 
         stack.enter_context(tc.manual_schedule())
-        for n in range(-H - X_LEAD - DMA_LEAD, STEPS + ATTEND_LAG + 2):
-            if is_step(n + QK_LEAD + DMA_LEAD) and (n + QK_LEAD + DMA_LEAD) % H == 0:
-                load_qk((n + QK_LEAD + DMA_LEAD) // H)
-            if -H <= n + X_LEAD + DMA_LEAD < STEPS and (n + X_LEAD + DMA_LEAD) % H == 0:
+        load_qk(0)
+        load_rows(-1)
+        load_rows(0)
+        load_qk(1)
+        load_rows(1)
+        prepare_qk(0)
+        make_mask_term(0)
+        scores(0, 0)
+        scores(0, 1)
+        for n in range(0, STEPS + ATTEND_LAG + 2):
+            if (n + 2 + DMA_LEAD) % H == 0 and 2 * H <= n + 2 + DMA_LEAD < STEPS:
+                load_qk((n + 2 + DMA_LEAD) // H)
+            if (n + X_LEAD + DMA_LEAD) % H == 0 and 2 * H <= n + X_LEAD + DMA_LEAD < STEPS:
                 load_rows((n + X_LEAD + DMA_LEAD) // H)
             for a in range(CHUNKS):
                 if is_step(n):
                     squash(n, a)
-                    if a % 2 == 1:
-                        add_mask_two(n, a // 2)
+                    for who, lo, hi in mask_plan(n):
+                        if who == "g" and a == hi - 1:
+                            add_mask(nc.gpsimd, n, lo, hi)
+                if a == 0 and is_step(n - EXP_LAG - 1) and scalar_takes_e1(n - EXP_LAG - 1):
+                    regroup_e(nc.scalar.copy, n - EXP_LAG - 1, 1)
                 ahead_n, ahead_a = divmod(n * CHUNKS + a + 2, CHUNKS)
                 if is_step(ahead_n):
                     scores(ahead_n, ahead_a)
-                if a == 3 and is_step(n - ATTEND_LAG):
-                    for j in range(CHUNKS):
-                        attend(n - ATTEND_LAG, j)
+                if n == 0 and a == 0:
+                    prepare_qk(1)
+                if a == 3:
+                    for m in attends(n):
+                        for j in range(CHUNKS):
+                            attend(m, j)
                 if a == 1:
                     for m in projects(n):
                         for j in range(CHUNKS):
                             project_v(m, j)
-                if a == 0 and is_step(n + QK_LEAD):
+                if a == (0 if n else 1) and is_step(n + 2):
                     for j in range(CHUNKS):
-                        transpose_qk(n + QK_LEAD, j)
+                        transpose_qk(n + 2, j)
                 if a == 2:
                     for slot in slots(n):
                         for j in range(CHUNKS):
                             transpose_x(slot, j)
                 if a == 3 and is_step(n + 1) and (n + 1) % H == 0:
                     make_mask_term((n + 1) // H)
-
                 if is_step(n - EXP_LAG):
                     exponential(n - EXP_LAG, a)
                     transpose_e(n - EXP_LAG, a)
-                if a == 2 and is_step(n + QK_LEAD):
-                    copy_qk(n + QK_LEAD)
+                if a == 2 and is_step(n + 2):
+                    copy_qk(n + 2)
+                if a == 2 and n >= STEPS:
+                    for m in projects(n):
+                        regroup_v(nc.scalar.copy, m)
             if is_step(n - EXP_LAG):
                 regroup_e(nc.scalar.copy, n - EXP_LAG, 0)
-            if is_step(n - EXP_LAG) and (False):
-                regroup_e(nc.scalar.copy, n - EXP_LAG, 1)
-            if is_step(n - EXP_LAG - 1):
+            if is_step(n - 1):
+                row_max(n - 1)
+            if is_step(n - EXP_LAG - 1) and not scalar_takes_e1(n - EXP_LAG - 1):
                 regroup_e(nc.vector.tensor_copy, n - EXP_LAG - 1, 1)
-            if is_step(n - ATTEND_LAG - 1):
-                invert_row_sum(n - ATTEND_LAG - 1)
-                normalise_and_store(n - ATTEND_LAG - 1)
-            if is_step(n - 1):
-                row_max(n - 1, 0)
+            for m in attends(n - 1):
+                normalise_and_store(m)
             for m in projects(n):
-                regroup_v(m)
-            if is_step(n - 1):
-                row_max(n - 1, 1)
+                if n < STEPS:
+                    regroup_v(nc.vector.tensor_copy, m)
+            for m in attends(n):
+                invert_row_sum(m)
             for slot in slots(n):
                 regroup_x(nc.vector.tensor_copy, slot)
+            if is_step(n):
+                for who, lo, hi in mask_plan(n):
+                    if who == "v":
+                        add_mask(nc.vector, n, lo, hi)
             if is_step(n - EXP_LAG - 1):
                 quantise_e(n - EXP_LAG - 1)
             for slot in slots(n):

@@ -175,9 +175,9 @@ def tile_attention_pa_t_kernel(tc, q, k, x, wv, mask, out):
                     ident_bf[:],
                 )
 
-        def copy_qk(n):
+        def copy_qk(copy, n):
             qk_t = qk_pool.tile([P, 2 * S], BF16)
-            nc.scalar.copy(out=qk_t[:], in_=live["qkt", n][:])
+            copy(out=qk_t[:], in_=live["qkt", n][:])
             live["qk_t", n] = qk_t
 
         def scores(n, a):
@@ -197,21 +197,20 @@ def tile_attention_pa_t_kernel(tc, q, k, x, wv, mask, out):
                 scale=1.0 / math.sqrt(DH),
             )
 
-        def add_mask(engine, n, lo, hi):
-            chunks = live["att", n][:, lo * S : hi * S].rearrange("p (a t) -> p a t", a=hi - lo)
-            term = live["mask_term", n // H][:].unsqueeze(1).to_broadcast([P, hi - lo, S])
-            engine.tensor_tensor(out=chunks, in0=chunks, in1=term, op=ALU.add)
+        def add_mask(n, pair):
+            two = live["att", n][:, pair * 2 * S : (pair + 1) * 2 * S].rearrange("p (a t) -> p a t", a=2)
+            term = live["mask_term", n // H][:].unsqueeze(1).to_broadcast([P, 2, S])
+            nc.gpsimd.tensor_tensor(out=two, in0=two, in1=term, op=ALU.add)
 
-        def row_max(n):
-            neg_max = soft.tile([P, CHUNKS], F32)
+        def row_max(n, pair):
+            if pair == 0:
+                neg_max = soft.tile([P, CHUNKS], F32)
+                live["neg_max", n] = neg_max
+            att = live["att", n][:].rearrange("p (a t) -> p a t", a=CHUNKS)
+            two = slice(2 * pair, 2 * pair + 2)
             nc.vector.tensor_reduce(
-                out=neg_max[:],
-                in_=live["att", n][:].rearrange("p (a t) -> p a t", a=CHUNKS),
-                axis=mybir.AxisListType.X,
-                op=ALU.max,
-                negate=True,
+                out=live["neg_max", n][:, two], in_=att[:, two, :], axis=mybir.AxisListType.X, op=ALU.max, negate=True
             )
-            live["neg_max", n] = neg_max
 
         def exponential(n, a):
             if a == 0:
@@ -293,7 +292,7 @@ def tile_attention_pa_t_kernel(tc, q, k, x, wv, mask, out):
         def is_step(n):
             return 0 <= n < STEPS
 
-        head_slots = {1: (-4, -3, -2, -1), 2: (0, 1, 2, 3), 3: (4,), 4: (5,)}
+        head_slots = {0: (-4, -3, -2, -1), 1: (0, 1), 2: (2, 3), 3: (4, 5)}
         head_projects = {3: (0, 1), 4: (2,), 5: (3,)}
 
         def slots(n):
@@ -305,16 +304,10 @@ def tile_attention_pa_t_kernel(tc, q, k, x, wv, mask, out):
         def attends(n):
             return [m for m in (n - ATTEND_LAG,) if is_step(m)]
 
-        def mask_plan(n):
-            return [("v" if n == 0 else "g", lo, lo + 2) for lo in (0, 2)]
-
-        def scalar_takes_e1(n):
-            return STEPS - EXP_LAG <= n < STEPS - 1
-
         def prepare_qk(n):
             for j in range(CHUNKS):
                 transpose_qk(n, j)
-            copy_qk(n)
+            copy_qk(nc.scalar.copy, n)
 
         stack.enter_context(tc.manual_schedule())
         load_qk(0)
@@ -334,10 +327,9 @@ def tile_attention_pa_t_kernel(tc, q, k, x, wv, mask, out):
             for a in range(CHUNKS):
                 if is_step(n):
                     squash(n, a)
-                    for who, lo, hi in mask_plan(n):
-                        if who == "g" and a == hi - 1:
-                            add_mask(nc.gpsimd, n, lo, hi)
-                if a == 0 and is_step(n - EXP_LAG - 1) and scalar_takes_e1(n - EXP_LAG - 1):
+                    if a % 2 == 1:
+                        add_mask(n, a // 2)
+                if a == 0 and is_step(n - EXP_LAG - 1):
                     regroup_e(nc.scalar.copy, n - EXP_LAG - 1, 1)
                 ahead_n, ahead_a = divmod(n * CHUNKS + a + 2, CHUNKS)
                 if is_step(ahead_n):
@@ -364,30 +356,26 @@ def tile_attention_pa_t_kernel(tc, q, k, x, wv, mask, out):
                 if is_step(n - EXP_LAG):
                     exponential(n - EXP_LAG, a)
                     transpose_e(n - EXP_LAG, a)
-                if a == 2 and is_step(n + 2):
-                    copy_qk(n + 2)
                 if a == 2 and n >= STEPS:
                     for m in projects(n):
                         regroup_v(nc.scalar.copy, m)
             if is_step(n - EXP_LAG):
                 regroup_e(nc.scalar.copy, n - EXP_LAG, 0)
-            if is_step(n - 1):
-                row_max(n - 1)
-            if is_step(n - EXP_LAG - 1) and not scalar_takes_e1(n - EXP_LAG - 1):
-                regroup_e(nc.vector.tensor_copy, n - EXP_LAG - 1, 1)
+            if is_step(n + 2):
+                copy_qk(nc.vector.tensor_copy, n + 2)
             for m in attends(n - 1):
                 normalise_and_store(m)
+            if is_step(n - 1):
+                row_max(n - 1, 0)
             for m in projects(n):
                 if n < STEPS:
                     regroup_v(nc.vector.tensor_copy, m)
+            if is_step(n - 1):
+                row_max(n - 1, 1)
             for m in attends(n):
                 invert_row_sum(m)
             for slot in slots(n):
                 regroup_x(nc.vector.tensor_copy, slot)
-            if is_step(n):
-                for who, lo, hi in mask_plan(n):
-                    if who == "v":
-                        add_mask(nc.vector, n, lo, hi)
             if is_step(n - EXP_LAG - 1):
                 quantise_e(n - EXP_LAG - 1)
             for slot in slots(n):

@@ -24,6 +24,7 @@ FLOPS = 2 * S * B * D * H * DH + 2 * 2 * B * H * S * S * DH
 X_LEAD = 2
 V_LAG = 2
 EXP_LAG = 2
+TURNED = 3
 ATTEND_LAG = 4
 DMA_LEAD = 4
 
@@ -43,7 +44,8 @@ def tile_attention_pa_t_kernel(tc, q, k, x, wv, mask, out):
         res = pool("res", 3)
         ps_s = psum("ps_s", 2)
         ps_et = psum("ps_et", 2)
-        ps_two = psum("ps_two", 2)
+        ps_two = psum("ps_two", 3)
+        ps_a = psum("ps_a", 1)
 
         ident_f32 = const.tile([P, P], F32)
         make_identity(nc, ident_f32[:])
@@ -51,6 +53,10 @@ def tile_attention_pa_t_kernel(tc, q, k, x, wv, mask, out):
         make_identity(nc, ident_bf[:])
         w_codes = const.tile([P, PASSES * S], U32, align_bytes=64)
         w_scales = const.tile([P, PASSES * S], U8, align_bytes=64)
+
+        mask_rows = const.tile([P, S], BF16)
+        nc.vector.memset(mask_rows[:], 0.0)
+        mask_cols = const.tile([P, CHUNKS * B], F32)
 
         live = {}
 
@@ -77,6 +83,20 @@ def tile_attention_pa_t_kernel(tc, q, k, x, wv, mask, out):
             )
             live["mask_term", b] = mask_term
 
+        def make_mask_cols():
+            mt = ps_two.tile([P, CHUNKS * P], BF16, tag="w")
+            for j in range(CHUNKS):
+                cols = slice(j * P, (j + 1) * P)
+                nc.tensor.transpose(mt[:, cols], mask_rows[:, cols], ident_bf[:])
+            nc.vector.tensor_scalar(
+                out=mask_cols[:].rearrange("p (j b) -> p j b", j=CHUNKS),
+                in0=mt[:].rearrange("p (j r) -> p j r", j=CHUNKS)[:, :, 0:B],
+                scalar1=10000.0,
+                scalar2=-10000.0,
+                op0=ALU.mult,
+                op1=ALU.add,
+            )
+
         def load_rows(b):
             x_sb = raw.tile([P, CHUNKS * D], BF16)
             slabs = x_sb[:].rearrange("p (j d) -> p j d", j=CHUNKS)
@@ -93,7 +113,7 @@ def tile_attention_pa_t_kernel(tc, q, k, x, wv, mask, out):
             g, pair = divmod(h, 2)
             u, s = divmod(quarter, 2)
             if quarter == 0:
-                xt = ps_two.tile([P, 512], F32, tag="x_or_v")
+                xt = ps_two.tile([P, 512], F32, tag="w")
                 live["xt", slot] = xt
             first = (2 * pair + s) * (D // 2) + (2 * g + u) * P
             nc.tensor.transpose(
@@ -134,7 +154,7 @@ def tile_attention_pa_t_kernel(tc, q, k, x, wv, mask, out):
         def project_v(n, j):
             b, h = divmod(n, H)
             if j == 0:
-                v_ps = ps_two.tile([P, CHUNKS * DH], F32, tag="x_or_v")
+                v_ps = ps_two.tile([P, CHUNKS * DH], F32, tag="w")
                 live["v_ps", n] = v_ps
             for g in range(PASSES):
                 rows = slice(g * S + j * P, g * S + (j + 1) * P)
@@ -166,7 +186,7 @@ def tile_attention_pa_t_kernel(tc, q, k, x, wv, mask, out):
         def transpose_qk(n, a):
             b, h = divmod(n, H)
             if a == 0:
-                qkt = ps_two.tile([P, 2 * S], BF16, tag="qk_or_o")
+                qkt = ps_two.tile([P, 2 * S], BF16, tag="w")
                 live["qkt", n] = qkt
             for which, rows_sb in enumerate((live["q_sb", b], live["k_sb", b])):
                 nc.tensor.transpose(
@@ -183,7 +203,13 @@ def tile_attention_pa_t_kernel(tc, q, k, x, wv, mask, out):
         def scores(n, a):
             qk_t = live["qk_t", n]
             s_ps = ps_s.tile([P, S], F32)
-            nc.tensor.matmul(s_ps[:], lhsT=qk_t[:, a * P : (a + 1) * P], rhs=qk_t[:, S : 2 * S], start=True, stop=True)
+            queries = qk_t[:, a * P : (a + 1) * P]
+            if a == TURNED:
+                for j in range(CHUNKS):
+                    keys = qk_t[:, S + j * P : S + (j + 1) * P]
+                    nc.tensor.matmul(s_ps[:, j * P : (j + 1) * P], lhsT=keys, rhs=queries, start=True, stop=True)
+            else:
+                nc.tensor.matmul(s_ps[:], lhsT=queries, rhs=qk_t[:, S : 2 * S], start=True, stop=True)
             live["s_ps", n, a] = s_ps
 
         def squash(n, a):
@@ -197,19 +223,52 @@ def tile_attention_pa_t_kernel(tc, q, k, x, wv, mask, out):
                 scale=1.0 / math.sqrt(DH),
             )
 
-        def add_mask(n, pair):
-            two = live["att", n][:, pair * 2 * S : (pair + 1) * 2 * S].rearrange("p (a t) -> p a t", a=2)
-            term = live["mask_term", n // H][:].unsqueeze(1).to_broadcast([P, 2, S])
-            nc.gpsimd.tensor_tensor(out=two, in0=two, in1=term, op=ALU.add)
+        def add_mask(n):
+            chunks = live["att", n][:, 0 : TURNED * S].rearrange("p (a t) -> p a t", a=TURNED)
+            term = live["mask_term", n // H][:].unsqueeze(1).to_broadcast([P, TURNED, S])
+            nc.gpsimd.tensor_tensor(out=chunks, in0=chunks, in1=term, op=ALU.add)
 
-        def row_max(n, pair):
-            if pair == 0:
-                neg_max = soft.tile([P, CHUNKS], F32)
-                live["neg_max", n] = neg_max
-            att = live["att", n][:].rearrange("p (a t) -> p a t", a=CHUNKS)
-            two = slice(2 * pair, 2 * pair + 2)
+        def turn_back(n):
+            a_ps = ps_a.tile([P, S], F32)
+            for j in range(CHUNKS):
+                cols = slice(j * P, (j + 1) * P)
+                first = TURNED * S + j * P
+                nc.tensor.matmul(
+                    a_ps[:, cols],
+                    lhsT=live["att", n][:, first : first + P],
+                    rhs=ident_f32[:],
+                    start=True,
+                    stop=False,
+                    is_transpose=True,
+                )
+                nc.tensor.matmul(
+                    a_ps[:, cols],
+                    lhsT=mask_cols[:, j * B + n // H : j * B + n // H + 1].to_broadcast([P, P]),
+                    rhs=ident_f32[:],
+                    start=False,
+                    stop=True,
+                    is_transpose=True,
+                )
+            live["a_ps", n] = a_ps
+
+        def row_max(n):
+            neg_max = soft.tile([P, CHUNKS], F32)
             nc.vector.tensor_reduce(
-                out=live["neg_max", n][:, two], in_=att[:, two, :], axis=mybir.AxisListType.X, op=ALU.max, negate=True
+                out=neg_max[:, 0:TURNED],
+                in_=live["att", n][:, 0 : TURNED * S].rearrange("p (a t) -> p a t", a=TURNED),
+                axis=mybir.AxisListType.X,
+                op=ALU.max,
+                negate=True,
+            )
+            live["neg_max", n] = neg_max
+
+        def row_max_turned(n):
+            nc.vector.tensor_reduce(
+                out=live["neg_max", n][:, TURNED : TURNED + 1],
+                in_=live["a_ps", n][:],
+                axis=mybir.AxisListType.X,
+                op=ALU.max,
+                negate=True,
             )
 
         def exponential(n, a):
@@ -219,7 +278,7 @@ def tile_attention_pa_t_kernel(tc, q, k, x, wv, mask, out):
                 live["e_sb", n], live["row_sum", n] = e_sb, row_sum
             nc.scalar.activation(
                 out=live["e_sb", n][:, a * S : (a + 1) * S],
-                in_=live["att", n][:, a * S : (a + 1) * S],
+                in_=live["a_ps", n][:] if a == TURNED else live["att", n][:, a * S : (a + 1) * S],
                 func=ACT.Exp,
                 bias=live["neg_max", n][:, a : a + 1],
                 scale=1.0,
@@ -257,7 +316,7 @@ def tile_attention_pa_t_kernel(tc, q, k, x, wv, mask, out):
 
         def attend(n, a):
             if a == 0:
-                o_ps = ps_two.tile([P, CHUNKS * DH], F32, tag="qk_or_o")
+                o_ps = ps_two.tile([P, CHUNKS * DH], F32, tag="w")
                 live["o_ps", n] = o_ps
             cols = slice(a * P, (a + 1) * P)
             nc.tensor.matmul_mx(
@@ -313,6 +372,7 @@ def tile_attention_pa_t_kernel(tc, q, k, x, wv, mask, out):
         load_qk(0)
         load_rows(-1)
         load_rows(0)
+        nc.sync.dma_start(out=mask_rows[0:B, :], in_=mask)
         load_qk(1)
         load_rows(1)
         prepare_qk(0)
@@ -327,13 +387,16 @@ def tile_attention_pa_t_kernel(tc, q, k, x, wv, mask, out):
             for a in range(CHUNKS):
                 if is_step(n):
                     squash(n, a)
-                    if a % 2 == 1:
-                        add_mask(n, a // 2)
+                    if a == TURNED - 1:
+                        add_mask(n)
                 if a == 0 and is_step(n - EXP_LAG - 1):
                     regroup_e(nc.scalar.copy, n - EXP_LAG - 1, 1)
                 ahead_n, ahead_a = divmod(n * CHUNKS + a + 2, CHUNKS)
                 if is_step(ahead_n):
                     scores(ahead_n, ahead_a)
+                if a == 0 and is_step(n - 2):
+                    turn_back(n - 2)
+                    row_max_turned(n - 2)
                 if n == 0 and a == 0:
                     prepare_qk(1)
                 if a == 3:
@@ -366,12 +429,10 @@ def tile_attention_pa_t_kernel(tc, q, k, x, wv, mask, out):
             for m in attends(n - 1):
                 normalise_and_store(m)
             if is_step(n - 1):
-                row_max(n - 1, 0)
+                row_max(n - 1)
             for m in projects(n):
                 if n < STEPS:
                     regroup_v(nc.vector.tensor_copy, m)
-            if is_step(n - 1):
-                row_max(n - 1, 1)
             for m in attends(n):
                 invert_row_sum(m)
             for slot in slots(n):
@@ -382,3 +443,5 @@ def tile_attention_pa_t_kernel(tc, q, k, x, wv, mask, out):
                 quantise_x(slot)
             for m in projects(n):
                 quantise_v(m)
+            if n == 1:
+                make_mask_cols()

@@ -41,7 +41,7 @@ def tile_attention_pa_t_kernel(tc, q, k, x, wv, mask, out):
         soft = pool("soft", 3)
         kept = pool("kept", 10)
         val = pool("val", 4)
-        res = pool("res", 3)
+        res = pool("res", 6)
         ps_s = psum("ps_s", 2)
         ps_et = psum("ps_et", 2)
         ps_two = psum("ps_two", 3)
@@ -63,7 +63,7 @@ def tile_attention_pa_t_kernel(tc, q, k, x, wv, mask, out):
         def load_qk(b):
             q_sb = raw.tile([P, H * S], BF16)
             k_sb = raw.tile([P, H * S], BF16)
-            for lo, hi in ((0, 1), (1, H)):
+            for lo, hi in ((0, 1), (1, 2), (2, H)) if b == 0 else ((0, H),):
                 nc.sync.dma_start(
                     out=q_sb[:, lo * S : hi * S].rearrange("p (h f) -> p h f", f=S),
                     in_=q[b, lo:hi].rearrange("h (p a) c -> p h (a c)", a=CHUNKS),
@@ -151,6 +151,17 @@ def tile_attention_pa_t_kernel(tc, q, k, x, wv, mask, out):
                     in_=live["x_grouped", b][:, g * 4 * S : (g + 1) * 4 * S],
                 )
 
+        def keep_warm(bank):
+            nc.tensor.matmul_mx(
+                out=bank[:],
+                lhsT=w_codes[:, 0:P].bitcast(FP8X4),
+                lhsT_scale=w_scales[:, 0:P],
+                rhs=w_codes[:, 0:S].bitcast(FP8X4),
+                rhs_scale=w_scales[:, 0:S],
+                start=True,
+                stop=True,
+            )
+
         def project_v(n, j):
             b, h = divmod(n, H)
             if j == 0:
@@ -223,13 +234,15 @@ def tile_attention_pa_t_kernel(tc, q, k, x, wv, mask, out):
                 scale=1.0 / math.sqrt(DH),
             )
 
-        def add_mask(n):
-            chunks = live["att", n][:, 0 : TURNED * S].rearrange("p (a t) -> p a t", a=TURNED)
-            term = live["mask_term", n // H][:].unsqueeze(1).to_broadcast([P, TURNED, S])
-            nc.gpsimd.tensor_tensor(out=chunks, in0=chunks, in1=term, op=ALU.add)
+        def add_mask(engine, n, lo, hi):
+            chunks = live["att", n][:, lo * S : hi * S].rearrange("p (a t) -> p a t", a=hi - lo)
+            term = live["mask_term", n // H][:].unsqueeze(1).to_broadcast([P, hi - lo, S])
+            engine.tensor_tensor(out=chunks, in0=chunks, in1=term, op=ALU.add)
 
         def turn_back(n):
             a_ps = ps_a.tile([P, S], F32)
+            if n > 1:
+                keep_warm(a_ps)
             for j in range(CHUNKS):
                 cols = slice(j * P, (j + 1) * P)
                 first = TURNED * S + j * P
@@ -308,11 +321,17 @@ def tile_attention_pa_t_kernel(tc, q, k, x, wv, mask, out):
                 in_=live["et", n, pair][:].rearrange("p (u c) -> p c u", u=2),
             )
 
-        def quantise_e(n):
-            e_codes = kept.tile([P, S], U32, align_bytes=64)
-            e_scales = kept.tile([P, S], U8, align_bytes=64)
-            nc.vector.quantize_mx(out=e_codes[:].bitcast(FP8X4), scales=e_scales[:], in_=live["e_grouped", n][:])
-            live["e_codes", n], live["e_scales", n] = e_codes, e_scales
+        def quantise_e(n, lo, hi):
+            if lo == 0:
+                e_codes = kept.tile([P, S], U32, align_bytes=64)
+                e_scales = kept.tile([P, S], U8, align_bytes=64)
+                live["e_codes", n], live["e_scales", n] = e_codes, e_scales
+            cols = slice(lo * P, hi * P)
+            nc.vector.quantize_mx(
+                out=live["e_codes", n][:, cols].bitcast(FP8X4),
+                scales=live["e_scales", n][:, cols],
+                in_=live["e_grouped", n][:, lo * S : hi * S],
+            )
 
         def attend(n, a):
             if a == 0:
@@ -334,19 +353,18 @@ def tile_attention_pa_t_kernel(tc, q, k, x, wv, mask, out):
             nc.vector.reciprocal(out=inv_sum[:], in_=live["row_sum", n][:])
             live["inv_sum", n] = inv_sum
 
-        def normalise_and_store(n):
+        def normalise_and_store(n, lo, hi):
             b, h = divmod(n, H)
-            o_sb = res.tile([P, CHUNKS * DH], F32)
-            o_view = o_sb[:].rearrange("p (a c) -> p a c", a=CHUNKS)
+            o_sb = res.tile([P, (hi - lo) * DH], F32, tag="o_sb")
+            o_view = o_sb[:].rearrange("p (a c) -> p a c", c=DH)
             nc.vector.tensor_tensor(
                 out=o_view,
-                in0=live["o_ps", n][:].rearrange("p (a c) -> p a c", a=CHUNKS),
-                in1=live["inv_sum", n][:].unsqueeze(2).to_broadcast([P, CHUNKS, DH]),
+                in0=live["o_ps", n][:, lo * DH : hi * DH].rearrange("p (a c) -> p a c", c=DH),
+                in1=live["inv_sum", n][:, lo:hi].unsqueeze(2).to_broadcast([P, hi - lo, DH]),
                 op=ALU.mult,
             )
-            nc.sync.dma_start(
-                out=out[:, b, h * DH : (h + 1) * DH].rearrange("(p a) c -> p a c", a=CHUNKS), in_=o_view
-            )
+            rows = out[:, b, h * DH : (h + 1) * DH].rearrange("(p a) c -> p a c", a=CHUNKS)
+            nc.sync.dma_start(out=rows[:, lo:hi, :], in_=o_view)
 
         def is_step(n):
             return 0 <= n < STEPS
@@ -370,16 +388,17 @@ def tile_attention_pa_t_kernel(tc, q, k, x, wv, mask, out):
 
         stack.enter_context(tc.manual_schedule())
         load_qk(0)
+        nc.sync.dma_start(out=mask_rows[0:B, :], in_=mask)
         load_rows(-1)
         load_rows(0)
-        nc.sync.dma_start(out=mask_rows[0:B, :], in_=mask)
         load_qk(1)
         load_rows(1)
         prepare_qk(0)
         make_mask_term(0)
         scores(0, 0)
         scores(0, 1)
-        for n in range(0, STEPS + ATTEND_LAG + 2):
+        make_mask_cols()
+        for n in range(STEPS + EXP_LAG):
             if (n + 2 + DMA_LEAD) % H == 0 and 2 * H <= n + 2 + DMA_LEAD < STEPS:
                 load_qk((n + 2 + DMA_LEAD) // H)
             if (n + X_LEAD + DMA_LEAD) % H == 0 and 2 * H <= n + X_LEAD + DMA_LEAD < STEPS:
@@ -387,8 +406,10 @@ def tile_attention_pa_t_kernel(tc, q, k, x, wv, mask, out):
             for a in range(CHUNKS):
                 if is_step(n):
                     squash(n, a)
-                    if a == TURNED - 1:
-                        add_mask(n)
+                    if n == 0 and a < TURNED:
+                        add_mask(nc.vector, n, a, a + 1)
+                    if n > 0 and a == TURNED - 1:
+                        add_mask(nc.gpsimd, n, 0, TURNED)
                 if a == 0 and is_step(n - EXP_LAG - 1):
                     regroup_e(nc.scalar.copy, n - EXP_LAG - 1, 1)
                 ahead_n, ahead_a = divmod(n * CHUNKS + a + 2, CHUNKS)
@@ -422,26 +443,43 @@ def tile_attention_pa_t_kernel(tc, q, k, x, wv, mask, out):
                 if a == 2 and n >= STEPS:
                     for m in projects(n):
                         regroup_v(nc.scalar.copy, m)
-            if is_step(n - EXP_LAG):
+            if 0 <= n - EXP_LAG < STEPS - 1:
                 regroup_e(nc.scalar.copy, n - EXP_LAG, 0)
             if is_step(n + 2):
                 copy_qk(nc.vector.tensor_copy, n + 2)
             for m in attends(n - 1):
-                normalise_and_store(m)
-            if is_step(n - 1):
-                row_max(n - 1)
+                normalise_and_store(m, 0, CHUNKS)
             for m in projects(n):
                 if n < STEPS:
                     regroup_v(nc.vector.tensor_copy, m)
+            if is_step(n - 1):
+                row_max(n - 1)
             for m in attends(n):
                 invert_row_sum(m)
             for slot in slots(n):
                 regroup_x(nc.vector.tensor_copy, slot)
             if is_step(n - EXP_LAG - 1):
-                quantise_e(n - EXP_LAG - 1)
+                quantise_e(n - EXP_LAG - 1, 0, CHUNKS)
             for slot in slots(n):
                 quantise_x(slot)
             for m in projects(n):
                 quantise_v(m)
-            if n == 1:
-                make_mask_cols()
+
+        last = STEPS - 1
+        half = CHUNKS // 2
+        regroup_e(nc.vector.tensor_copy, last, 0)
+        regroup_e(nc.scalar.copy, last, 1)
+        normalise_and_store(last - 2, 0, CHUNKS)
+        invert_row_sum(last - 1)
+        quantise_e(last, 0, half)
+        for a in range(CHUNKS):
+            attend(last - 1, a)
+        for a in range(half):
+            attend(last, a)
+        invert_row_sum(last)
+        normalise_and_store(last - 1, 0, CHUNKS)
+        normalise_and_store(last, 0, half)
+        quantise_e(last, half, CHUNKS)
+        for a in range(half, CHUNKS):
+            attend(last, a)
+        normalise_and_store(last, half, CHUNKS)

@@ -21,12 +21,28 @@ STEPS = B * H
 
 FLOPS = 2 * S * B * D * H * DH + 2 * 2 * B * H * S * S * DH
 
-X_LEAD = 2
+X_LEAD = 3
 V_LAG = 2
 EXP_LAG = 2
 TURNED = 3
-ATTEND_LAG = 4
+ATTEND_LAG = 3
 DMA_LEAD = 4
+SOFT = 4
+HS = {1: (-4, -3, -2, -1), 2: (0, 1), 3: (2, 3), 4: (4, 5), 5: (6, 7), 6: (8, 9)}
+SS = 10
+HP = {5: (0, 1), 6: (2, 3), 7: (4, 5)}
+PS = 6
+HA = {6: (0, 1), 7: (2, 3), 8: (4, 5)}
+W0 = False
+SV = False
+TC = False
+WS = (1,)
+WH = (0, 1, 3)
+NH = 7
+VA = {1: "XV|012|q", 32: "t0|VE12vi|o", 33: "t|VEvi|o"}
+SW = ()
+MG = 0
+LG = ()
 
 
 def tile_attention_pa_t_kernel(tc, q, k, x, wv, mask, out):
@@ -35,10 +51,10 @@ def tile_attention_pa_t_kernel(tc, q, k, x, wv, mask, out):
         pool = lambda name, bufs: stack.enter_context(tc.tile_pool(name=name, bufs=bufs))
         psum = lambda name, bufs: stack.enter_context(tc.psum_pool(name=name, bufs=bufs))
         const = pool("const", 1)
-        raw = pool("raw", 2)
+        raw = pool("raw", 3)
         proj = pool("proj", 2)
         qk_pool = pool("qk", 4)
-        soft = pool("soft", 3)
+        soft = pool("soft", SOFT)
         kept = pool("kept", 10)
         val = pool("val", 4)
         res = pool("res", 6)
@@ -63,6 +79,7 @@ def tile_attention_pa_t_kernel(tc, q, k, x, wv, mask, out):
         def load_qk(b):
             q_sb = raw.tile([P, H * S], BF16)
             k_sb = raw.tile([P, H * S], BF16)
+            mask_sb = raw.tile([P, S], BF16)
             for lo, hi in ((0, 1), (1, 2), (2, H)) if b == 0 else ((0, H),):
                 nc.sync.dma_start(
                     out=q_sb[:, lo * S : hi * S].rearrange("p (h f) -> p h f", f=S),
@@ -72,13 +89,15 @@ def tile_attention_pa_t_kernel(tc, q, k, x, wv, mask, out):
                     out=k_sb[:, lo * S : hi * S].rearrange("p (f c) -> p f c", c=DH),
                     in_=k[b, lo:hi].rearrange("h (a p) c -> p (h a) c", p=P),
                 )
-            mask_sb = raw.tile([P, S], BF16)
-            nc.sync.dma_start(out=mask_sb[:], in_=mask[b].partition_broadcast(P))
+                if lo == 0:
+                    nc.sync.dma_start(out=mask_sb[:], in_=mask[b].partition_broadcast(P))
+                    if b == 0:
+                        nc.sync.dma_start(out=mask_rows[0:B, :], in_=mask)
             live["q_sb", b], live["k_sb", b], live["mask_sb", b] = q_sb, k_sb, mask_sb
 
         def make_mask_term(b):
             mask_term = raw.tile([P, S], F32)
-            nc.vector.tensor_scalar(
+            (nc.gpsimd if b and MG else nc.vector).tensor_scalar(
                 out=mask_term[:], in0=live["mask_sb", b][:], scalar1=10000.0, scalar2=-10000.0, op0=ALU.mult, op1=ALU.add
             )
             live["mask_term", b] = mask_term
@@ -213,7 +232,9 @@ def tile_attention_pa_t_kernel(tc, q, k, x, wv, mask, out):
 
         def scores(n, a):
             qk_t = live["qk_t", n]
-            s_ps = ps_s.tile([P, S], F32)
+            s_ps = ps_s.tile([P, S], F32, tag="s")
+            if n > 2 and a in (WS if n >= NH else WH):
+                keep_warm(s_ps)
             queries = qk_t[:, a * P : (a + 1) * P]
             if a == TURNED:
                 for j in range(CHUNKS):
@@ -241,7 +262,7 @@ def tile_attention_pa_t_kernel(tc, q, k, x, wv, mask, out):
 
         def turn_back(n):
             a_ps = ps_a.tile([P, S], F32)
-            if n > 1:
+            if n > 1 and W0:
                 keep_warm(a_ps)
             for j in range(CHUNKS):
                 cols = slice(j * P, (j + 1) * P)
@@ -264,16 +285,17 @@ def tile_attention_pa_t_kernel(tc, q, k, x, wv, mask, out):
                 )
             live["a_ps", n] = a_ps
 
-        def row_max(n):
-            neg_max = soft.tile([P, CHUNKS], F32)
+        def row_max(n, lo=0, hi=TURNED):
+            if lo == 0:
+                neg_max = soft.tile([P, CHUNKS], F32)
+                live["neg_max", n] = neg_max
             nc.vector.tensor_reduce(
-                out=neg_max[:, 0:TURNED],
-                in_=live["att", n][:, 0 : TURNED * S].rearrange("p (a t) -> p a t", a=TURNED),
+                out=live["neg_max", n][:, lo:hi],
+                in_=live["att", n][:, lo * S : hi * S].rearrange("p (a t) -> p a t", a=hi - lo),
                 axis=mybir.AxisListType.X,
                 op=ALU.max,
                 negate=True,
             )
-            live["neg_max", n] = neg_max
 
         def row_max_turned(n):
             nc.vector.tensor_reduce(
@@ -333,10 +355,12 @@ def tile_attention_pa_t_kernel(tc, q, k, x, wv, mask, out):
                 in_=live["e_grouped", n][:, lo * S : hi * S],
             )
 
-        def attend(n, a):
+        def attend(n, a, warm=False):
             if a == 0:
                 o_ps = ps_two.tile([P, CHUNKS * DH], F32, tag="w")
                 live["o_ps", n] = o_ps
+            if warm:
+                keep_warm(live["o_ps", n])
             cols = slice(a * P, (a + 1) * P)
             nc.tensor.matmul_mx(
                 out=live["o_ps", n][:, a * DH : (a + 1) * DH],
@@ -369,115 +393,161 @@ def tile_attention_pa_t_kernel(tc, q, k, x, wv, mask, out):
         def is_step(n):
             return 0 <= n < STEPS
 
-        head_slots = {0: (-4, -3, -2, -1), 1: (0, 1), 2: (2, 3), 3: (4, 5)}
-        head_projects = {3: (0, 1), 4: (2,), 5: (3,)}
-
         def slots(n):
-            return list(head_slots.get(n, ())) + [s for s in (n + X_LEAD,) if 6 <= s < STEPS]
+            return list(HS.get(n, ())) + [s for s in (n + X_LEAD,) if SS <= s < STEPS]
 
         def projects(n):
-            return list(head_projects.get(n, ())) + [m for m in (n - V_LAG,) if 4 <= m < STEPS]
+            return list(HP.get(n, ())) + [m for m in (n - V_LAG,) if PS <= m < STEPS]
 
         def attends(n):
-            return [m for m in (n - ATTEND_LAG,) if is_step(m)]
+            return list(HA.get(n, ())) + [m for m in (n - ATTEND_LAG,) if PS <= m < STEPS]
 
-        def prepare_qk(n):
+        def prepare_qk(n, copy):
             for j in range(CHUNKS):
                 transpose_qk(n, j)
-            copy_qk(nc.scalar.copy, n)
+            copy_qk(copy, n)
+
+        def scores_ahead(n, a):
+            n, a = divmod(n * CHUNKS + a + 2, CHUNKS)
+            if is_step(n):
+                scores(n, a)
+
+        def exp_chunk(n, a):
+            if is_step(n):
+                exponential(n, a)
+                transpose_e(n, a)
 
         stack.enter_context(tc.manual_schedule())
         load_qk(0)
-        nc.sync.dma_start(out=mask_rows[0:B, :], in_=mask)
         load_rows(-1)
         load_rows(0)
         load_qk(1)
         load_rows(1)
-        prepare_qk(0)
+        prepare_qk(0, nc.scalar.copy)
         make_mask_term(0)
         scores(0, 0)
         scores(0, 1)
         make_mask_cols()
+        def vector_work(n, order):
+            for piece in order:
+                if piece == "X":
+                    for slot in slots(n - 1):
+                        quantise_x(slot)
+                if piece == "V":
+                    for m in projects(n - 1):
+                        quantise_v(m)
+                if piece == "E" and is_step(n - EXP_LAG - 1):
+                    quantise_e(n - EXP_LAG - 1, 0, CHUNKS)
+                if piece == "v":
+                    for m in projects(n):
+                        regroup_v(nc.vector.tensor_copy, m)
+                if piece == "i":
+                    for m in attends(n):
+                        invert_row_sum(m)
+                if piece in "012" and is_step(n - 1):
+                    row_max(n - 1, int(piece), int(piece) + 1)
+                if piece == "m" and is_step(n - 1):
+                    row_max(n - 1, 1, 3)
+                if piece == "t" and is_step(n - 2):
+                    row_max_turned(n - 2)
+                if piece == "x":
+                    for slot in slots(n)[0:1] if n > 1 else ():
+                        regroup_x(nc.vector.tensor_copy, slot)
+                if piece == "o":
+                    for m in attends(n):
+                        normalise_and_store(m, 0, CHUNKS)
+                if piece == "q" and is_step(n + 2):
+                    copy_qk(nc.vector.tensor_copy, n + 2)
+
         for n in range(STEPS + EXP_LAG):
             if (n + 2 + DMA_LEAD) % H == 0 and 2 * H <= n + 2 + DMA_LEAD < STEPS:
                 load_qk((n + 2 + DMA_LEAD) // H)
             if (n + X_LEAD + DMA_LEAD) % H == 0 and 2 * H <= n + X_LEAD + DMA_LEAD < STEPS:
                 load_rows((n + X_LEAD + DMA_LEAD) // H)
-            for a in range(CHUNKS):
-                if is_step(n):
-                    squash(n, a)
-                    if n == 0 and a < TURNED:
-                        add_mask(nc.vector, n, a, a + 1)
-                    if n > 0 and a == TURNED - 1:
-                        add_mask(nc.gpsimd, n, 0, TURNED)
-                if a == 0 and is_step(n - EXP_LAG - 1):
-                    regroup_e(nc.scalar.copy, n - EXP_LAG - 1, 1)
-                ahead_n, ahead_a = divmod(n * CHUNKS + a + 2, CHUNKS)
-                if is_step(ahead_n):
-                    scores(ahead_n, ahead_a)
-                if a == 0 and is_step(n - 2):
-                    turn_back(n - 2)
-                    row_max_turned(n - 2)
-                if n == 0 and a == 0:
-                    prepare_qk(1)
-                if a == 3:
-                    for m in attends(n):
-                        for j in range(CHUNKS):
-                            attend(m, j)
-                if a == 1:
-                    for m in projects(n):
-                        for j in range(CHUNKS):
-                            project_v(m, j)
-                if a == (0 if n else 1) and is_step(n + 2):
+            if is_step(n):
+                squash(n, 0)
+                if n == 0:
+                    add_mask(nc.vector, n, 0, 1)
+            scores_ahead(n, 0)
+            if n == 0:
+                prepare_qk(1, nc.vector.tensor_copy)
+            if n >= STEPS:
+                turn_back(n - 2)
+            if n in VA:
+                for c in VA[n].split("|")[0]:
+                    vector_work(n, c)
+            else:
+                vector_work(n, "XV")
+            for m in projects(n):
+                for j in range(CHUNKS):
+                    project_v(m, j)
+            if n > 1:
+                for slot in slots(n)[:1]:
                     for j in range(CHUNKS):
-                        transpose_qk(n + 2, j)
-                if a == 2:
-                    for slot in slots(n):
-                        for j in range(CHUNKS):
-                            transpose_x(slot, j)
-                if a == 3 and is_step(n + 1) and (n + 1) % H == 0:
-                    make_mask_term((n + 1) // H)
-                if is_step(n - EXP_LAG):
-                    exponential(n - EXP_LAG, a)
-                    transpose_e(n - EXP_LAG, a)
-                if a == 2 and n >= STEPS:
-                    for m in projects(n):
-                        regroup_v(nc.scalar.copy, m)
+                        transpose_x(slot, j)
+            exp_chunk(n - EXP_LAG, 0)
+            if is_step(n - EXP_LAG - 1):
+                regroup_e(nc.scalar.copy, n - EXP_LAG - 1, 1)
+            if n == STEPS - 1 and 0 in LG:
+                add_mask(nc.gpsimd, n, 0, 1)
+            if is_step(n):
+                squash(n, 1)
+                if n == STEPS - 1 and 1 in LG:
+                    add_mask(nc.gpsimd, n, 1, 2)
+                if n == 0:
+                    add_mask(nc.vector, n, 1, 2)
+            scores_ahead(n, 1)
+            if is_step(n - 2) and n < STEPS:
+                turn_back(n - 2)
+            exp_chunk(n - EXP_LAG, 1)
+            vector_work(n, VA[n].split("|")[1] if n in VA else "Evi0t")
+            if is_step(n):
+                squash(n, 2)
+                if n == 0:
+                    add_mask(nc.vector, n, 2, 3)
+                elif n < STEPS - 1:
+                    add_mask(nc.gpsimd, n, 0, TURNED)
+                if MG and n % H == MG and n < STEPS - H:
+                    make_mask_term(n // H + 1)
+            if n == STEPS - 1 and 2 in LG:
+                add_mask(nc.gpsimd, n, 2, 3)
+            scores_ahead(n, 2)
+            vector_work(n, "x")
+            for k2, slot in enumerate(slots(n)[1 if n > 1 else 0 :]):
+                for j in range(CHUNKS):
+                    transpose_x(slot, j)
+                regroup_x(nc.scalar.copy if n == 1 and k2 in SW else nc.vector.tensor_copy, slot)
+            for m in attends(n):
+                for j in range(CHUNKS):
+                    attend(m, j)
+            if is_step(n + 2):
+                for j in range(CHUNKS):
+                    transpose_qk(n + 2, j)
+            exp_chunk(n - EXP_LAG, 2)
+            vector_work(n, VA[n].split("|")[2] if n in VA else "oqm")
+            if n == STEPS - 1:
+                for a in range(TURNED):
+                    if a not in LG:
+                        add_mask(nc.vector, n, a, a + 1)
             if 0 <= n - EXP_LAG < STEPS - 1:
                 regroup_e(nc.scalar.copy, n - EXP_LAG, 0)
-            if is_step(n + 2):
-                copy_qk(nc.vector.tensor_copy, n + 2)
-            for m in attends(n - 1):
-                normalise_and_store(m, 0, CHUNKS)
-            for m in projects(n):
-                if n < STEPS:
-                    regroup_v(nc.vector.tensor_copy, m)
-            if is_step(n - 1):
-                row_max(n - 1)
-            for m in attends(n):
-                invert_row_sum(m)
-            for slot in slots(n):
-                regroup_x(nc.vector.tensor_copy, slot)
-            if is_step(n - EXP_LAG - 1):
-                quantise_e(n - EXP_LAG - 1, 0, CHUNKS)
-            for slot in slots(n):
-                quantise_x(slot)
-            for m in projects(n):
-                quantise_v(m)
+            if is_step(n):
+                squash(n, 3)
+            scores_ahead(n, 3)
+            if is_step(n + 1) and (n + 1) % H == 0 and MG == 0:
+                make_mask_term((n + 1) // H)
+            exp_chunk(n - EXP_LAG, 3)
 
         last = STEPS - 1
         half = CHUNKS // 2
         regroup_e(nc.vector.tensor_copy, last, 0)
         regroup_e(nc.scalar.copy, last, 1)
-        normalise_and_store(last - 2, 0, CHUNKS)
-        invert_row_sum(last - 1)
+        for m in projects(STEPS + EXP_LAG - 1):
+            quantise_v(m)
         quantise_e(last, 0, half)
-        for a in range(CHUNKS):
-            attend(last - 1, a)
         for a in range(half):
             attend(last, a)
         invert_row_sum(last)
-        normalise_and_store(last - 1, 0, CHUNKS)
         normalise_and_store(last, 0, half)
         quantise_e(last, half, CHUNKS)
         for a in range(half, CHUNKS):

@@ -21,28 +21,24 @@ STEPS = B * H
 
 FLOPS = 2 * S * B * D * H * DH + 2 * 2 * B * H * S * S * DH
 
-X_LEAD = 3
-V_LAG = 2
 EXP_LAG = 2
 TURNED = 3
-ATTEND_LAG = 3
 DMA_LEAD = 4
 SOFT = 4
-HS = {1: (-4, -3, -2, -1), 2: (0, 1), 3: (2, 3), 4: (4, 5), 5: (6, 7), 6: (8, 9)}
-SS = 10
-HP = {5: (0, 1), 6: (2, 3), 7: (4, 5)}
-PS = 6
-HA = {6: (0, 1), 7: (2, 3), 8: (4, 5)}
-W0 = False
-SV = False
-TC = False
+XW = 1
+XD = (2, 3, 4, 5, 6)
+P0 = 5
+DP = (5, 6, 7, 30, 31)
+A0 = 6
+DA = (6, 7, 8)
 WS = (1,)
 WH = (0, 1, 3)
 NH = 7
-VA = {1: "XV|012|q", 32: "t0|VE12vi|o", 33: "t|VEvi|o"}
-SW = ()
-MG = 0
-LG = ()
+ROWS_AT = (1, 5, 9, 13, 17, 21)
+NDUM = (3, 1, 0)
+LASTSPLIT = 2
+CV = ()
+FIN = True
 
 
 def tile_attention_pa_t_kernel(tc, q, k, x, wv, mask, out):
@@ -70,6 +66,8 @@ def tile_attention_pa_t_kernel(tc, q, k, x, wv, mask, out):
         w_codes = const.tile([P, PASSES * S], U32, align_bytes=64)
         w_scales = const.tile([P, PASSES * S], U8, align_bytes=64)
 
+        zeros = const.tile([P, S], BF16)
+        nc.vector.memset(zeros[:], 0.0)
         mask_rows = const.tile([P, S], BF16)
         nc.vector.memset(mask_rows[:], 0.0)
         mask_cols = const.tile([P, CHUNKS * B], F32)
@@ -97,7 +95,7 @@ def tile_attention_pa_t_kernel(tc, q, k, x, wv, mask, out):
 
         def make_mask_term(b):
             mask_term = raw.tile([P, S], F32)
-            (nc.gpsimd if b and MG else nc.vector).tensor_scalar(
+            nc.vector.tensor_scalar(
                 out=mask_term[:], in0=live["mask_sb", b][:], scalar1=10000.0, scalar2=-10000.0, op0=ALU.mult, op1=ALU.add
             )
             live["mask_term", b] = mask_term
@@ -233,7 +231,7 @@ def tile_attention_pa_t_kernel(tc, q, k, x, wv, mask, out):
         def scores(n, a):
             qk_t = live["qk_t", n]
             s_ps = ps_s.tile([P, S], F32, tag="s")
-            if n > 2 and a in (WS if n >= NH else WH):
+            if n > 3 and a in (WS if n >= NH else WH):
                 keep_warm(s_ps)
             queries = qk_t[:, a * P : (a + 1) * P]
             if a == TURNED:
@@ -261,9 +259,10 @@ def tile_attention_pa_t_kernel(tc, q, k, x, wv, mask, out):
             engine.tensor_tensor(out=chunks, in0=chunks, in1=term, op=ALU.add)
 
         def turn_back(n):
-            a_ps = ps_a.tile([P, S], F32)
-            if n > 1 and W0:
-                keep_warm(a_ps)
+            if n < STEPS - 2:
+                a_ps = ps_a.tile([P, S], F32, tag="a")
+            else:
+                a_ps = ps_s.tile([P, S], F32, tag="s")
             for j in range(CHUNKS):
                 cols = slice(j * P, (j + 1) * P)
                 first = TURNED * S + j * P
@@ -355,12 +354,10 @@ def tile_attention_pa_t_kernel(tc, q, k, x, wv, mask, out):
                 in_=live["e_grouped", n][:, lo * S : hi * S],
             )
 
-        def attend(n, a, warm=False):
+        def attend(n, a):
             if a == 0:
                 o_ps = ps_two.tile([P, CHUNKS * DH], F32, tag="w")
                 live["o_ps", n] = o_ps
-            if warm:
-                keep_warm(live["o_ps", n])
             cols = slice(a * P, (a + 1) * P)
             nc.tensor.matmul_mx(
                 out=live["o_ps", n][:, a * DH : (a + 1) * DH],
@@ -393,14 +390,28 @@ def tile_attention_pa_t_kernel(tc, q, k, x, wv, mask, out):
         def is_step(n):
             return 0 <= n < STEPS
 
+        def spread(first, turn, doubles):
+            plan, item = {}, first
+            while item < STEPS:
+                count = 2 if turn in doubles else 1
+                plan[turn] = [i for i in range(item, item + count) if i < STEPS]
+                item += count
+                turn += 1
+            return plan
+
+        x_plan = spread(0, XW + 1, XD)
+        x_plan[XW] = [-4, -3, -2, -1]
+        v_plan = spread(0, P0, DP)
+        o_plan = spread(0, A0, DA)
+
         def slots(n):
-            return list(HS.get(n, ())) + [s for s in (n + X_LEAD,) if SS <= s < STEPS]
+            return x_plan.get(n, [])
 
         def projects(n):
-            return list(HP.get(n, ())) + [m for m in (n - V_LAG,) if PS <= m < STEPS]
+            return v_plan.get(n, [])
 
         def attends(n):
-            return list(HA.get(n, ())) + [m for m in (n - ATTEND_LAG,) if PS <= m < STEPS]
+            return o_plan.get(n, [])
 
         def prepare_qk(n, copy):
             for j in range(CHUNKS):
@@ -417,17 +428,11 @@ def tile_attention_pa_t_kernel(tc, q, k, x, wv, mask, out):
                 exponential(n, a)
                 transpose_e(n, a)
 
-        stack.enter_context(tc.manual_schedule())
-        load_qk(0)
-        load_rows(-1)
-        load_rows(0)
-        load_qk(1)
-        load_rows(1)
-        prepare_qk(0, nc.scalar.copy)
-        make_mask_term(0)
-        scores(0, 0)
-        scores(0, 1)
-        make_mask_cols()
+        def move_x(copy, slot):
+            for j in range(CHUNKS):
+                transpose_x(slot, j)
+            regroup_x(copy, slot)
+
         def vector_work(n, order):
             for piece in order:
                 if piece == "X":
@@ -448,102 +453,141 @@ def tile_attention_pa_t_kernel(tc, q, k, x, wv, mask, out):
                     row_max(n - 1, int(piece), int(piece) + 1)
                 if piece == "m" and is_step(n - 1):
                     row_max(n - 1, 1, 3)
+                if piece == "M" and is_step(n - 1):
+                    row_max(n - 1, 0, 3)
+                if piece == "x" and n != XW:
+                    for slot in slots(n)[:1]:
+                        regroup_x(nc.vector.tensor_copy, slot)
                 if piece == "t" and is_step(n - 2):
                     row_max_turned(n - 2)
-                if piece == "x":
-                    for slot in slots(n)[0:1] if n > 1 else ():
-                        regroup_x(nc.vector.tensor_copy, slot)
                 if piece == "o":
                     for m in attends(n):
                         normalise_and_store(m, 0, CHUNKS)
-                if piece == "q" and is_step(n + 2):
+                if piece == "q" and is_step(n + 2) and n != 1:
                     copy_qk(nc.vector.tensor_copy, n + 2)
 
+        def dummy(count):
+            for i in range(count):
+                bank = ps_s.tile([P, S], F32, tag="s")
+                nc.tensor.matmul(bank[:], lhsT=zeros[:, 0:P], rhs=zeros[:], start=True, stop=True)
+
+        stack.enter_context(tc.manual_schedule())
+        load_qk(0)
+        load_rows(-1)
+        load_rows(0)
+        load_qk(1)
+        load_rows(1)
+        dummy(NDUM[0])
+        for j in range(CHUNKS):
+            transpose_qk(0, j)
+        copy_qk(nc.scalar.copy, 0)
+        dummy(NDUM[1])
+        make_mask_term(0)
+        scores(0, 0)
+        scores(0, 1)
+        for j in range(CHUNKS):
+            transpose_qk(1, j)
+        make_mask_cols()
         for n in range(STEPS + EXP_LAG):
             if (n + 2 + DMA_LEAD) % H == 0 and 2 * H <= n + 2 + DMA_LEAD < STEPS:
                 load_qk((n + 2 + DMA_LEAD) // H)
-            if (n + X_LEAD + DMA_LEAD) % H == 0 and 2 * H <= n + X_LEAD + DMA_LEAD < STEPS:
-                load_rows((n + X_LEAD + DMA_LEAD) // H)
+            if n in ROWS_AT:
+                load_rows(2 + ROWS_AT.index(n))
             if is_step(n):
                 squash(n, 0)
                 if n == 0:
                     add_mask(nc.vector, n, 0, 1)
             scores_ahead(n, 0)
             if n == 0:
-                prepare_qk(1, nc.vector.tensor_copy)
-            if n >= STEPS:
-                turn_back(n - 2)
-            if n in VA:
-                for c in VA[n].split("|")[0]:
-                    vector_work(n, c)
-            else:
+                copy_qk(nc.vector.tensor_copy, 1)
+            if n == STEPS:
+                turn_back(n - 1)
+            if n == 1:
+                vector_work(n, "012")
+            elif 2 < n < STEPS:
                 vector_work(n, "XV")
-            for m in projects(n):
+            if n == 2:
                 for j in range(CHUNKS):
-                    project_v(m, j)
-            if n > 1:
+                    transpose_qk(3, j)
+                copy_qk(nc.vector.tensor_copy, 3)
+            if n == STEPS:
+                vector_work(n, "m")
+                row_max_turned(n - 1)
+            if n < STEPS:
+                for m in projects(n):
+                    for j in range(CHUNKS):
+                        project_v(m, j)
+            if n > XW:
                 for slot in slots(n)[:1]:
                     for j in range(CHUNKS):
                         transpose_x(slot, j)
             exp_chunk(n - EXP_LAG, 0)
             if is_step(n - EXP_LAG - 1):
-                regroup_e(nc.scalar.copy, n - EXP_LAG - 1, 1)
-            if n == STEPS - 1 and 0 in LG:
-                add_mask(nc.gpsimd, n, 0, 1)
+                regroup_e(nc.vector.tensor_copy if n in CV else nc.scalar.copy, n - EXP_LAG - 1, 1)
             if is_step(n):
                 squash(n, 1)
-                if n == STEPS - 1 and 1 in LG:
-                    add_mask(nc.gpsimd, n, 1, 2)
+                if n == STEPS - 1:
+                    add_mask(nc.gpsimd, n, 0, LASTSPLIT)
                 if n == 0:
                     add_mask(nc.vector, n, 1, 2)
             scores_ahead(n, 1)
-            if is_step(n - 2) and n < STEPS:
+            if 2 < n < STEPS:
                 turn_back(n - 2)
             exp_chunk(n - EXP_LAG, 1)
-            vector_work(n, VA[n].split("|")[1] if n in VA else "Evi0t")
+            vector_work(n, "" if n == 1 else "0" if n == 2 else "VEvi" if n == STEPS else "Ei" if n > STEPS else "Evi0t")
             if is_step(n):
                 squash(n, 2)
                 if n == 0:
                     add_mask(nc.vector, n, 2, 3)
                 elif n < STEPS - 1:
                     add_mask(nc.gpsimd, n, 0, TURNED)
-                if MG and n % H == MG and n < STEPS - H:
-                    make_mask_term(n // H + 1)
-            if n == STEPS - 1 and 2 in LG:
-                add_mask(nc.gpsimd, n, 2, 3)
             scores_ahead(n, 2)
-            vector_work(n, "x")
-            for k2, slot in enumerate(slots(n)[1 if n > 1 else 0 :]):
-                for j in range(CHUNKS):
-                    transpose_x(slot, j)
-                regroup_x(nc.scalar.copy if n == 1 and k2 in SW else nc.vector.tensor_copy, slot)
-            for m in attends(n):
-                for j in range(CHUNKS):
-                    attend(m, j)
-            if is_step(n + 2):
+            if n == XW:
+                turn_back(0)
+                row_max_turned(0)
+                for slot in slots(n)[:3]:
+                    move_x(nc.vector.tensor_copy, slot)
+            else:
+                vector_work(n, "x")
+                for slot in slots(n)[1:]:
+                    move_x(nc.vector.tensor_copy, slot)
+            if n < STEPS:
+                for m in attends(n):
+                    for j in range(CHUNKS):
+                        attend(m, j)
+            if is_step(n + 2) and n != XW:
                 for j in range(CHUNKS):
                     transpose_qk(n + 2, j)
             exp_chunk(n - EXP_LAG, 2)
-            vector_work(n, VA[n].split("|")[2] if n in VA else "oqm")
+            vector_work(n, "" if n == XW or n >= STEPS else "qmX" if n == 2 else "oqm")
             if n == STEPS - 1:
-                for a in range(TURNED):
-                    if a not in LG:
-                        add_mask(nc.vector, n, a, a + 1)
+                if LASTSPLIT < 3:
+                    add_mask(nc.vector, n, LASTSPLIT, 3)
+                row_max(n, 0, 1)
             if 0 <= n - EXP_LAG < STEPS - 1:
                 regroup_e(nc.scalar.copy, n - EXP_LAG, 0)
             if is_step(n):
                 squash(n, 3)
             scores_ahead(n, 3)
-            if is_step(n + 1) and (n + 1) % H == 0 and MG == 0:
+            if n == XW:
+                for slot in slots(n)[3:]:
+                    move_x(nc.vector.tensor_copy, slot)
+            if n == STEPS - 1:
+                turn_back(n - 1)
+                row_max_turned(n - 1)
+            if is_step(n + 1) and (n + 1) % H == 0:
                 make_mask_term((n + 1) // H)
             exp_chunk(n - EXP_LAG, 3)
+            if n >= STEPS:
+                for m in attends(n):
+                    for j in range(CHUNKS):
+                        attend(m, j)
+                vector_work(n, "o")
 
         last = STEPS - 1
         half = CHUNKS // 2
-        regroup_e(nc.vector.tensor_copy, last, 0)
+        regroup_e(nc.scalar.copy if FIN else nc.vector.tensor_copy, last, 0)
         regroup_e(nc.scalar.copy, last, 1)
-        for m in projects(STEPS + EXP_LAG - 1):
-            quantise_v(m)
         quantise_e(last, 0, half)
         for a in range(half):
             attend(last, a)

@@ -24,13 +24,17 @@ FLOPS = 2 * S * B * D * H * DH + 2 * 2 * B * H * S * S * DH
 EXP_LAG = 2
 TURNED = 3
 DMA_LEAD = 4
-SOFT = 4
-XW = 1
+SOFT = 5
+X0 = 2
 XD = (2, 3, 4, 5, 6)
+G0 = True
+WEARLY = False
+WE = 2
+WL = 3
 P0 = 5
 DP = (5, 6, 7, 30, 31)
-A0 = 6
-DA = (6, 7, 8)
+A0 = 7
+DA = (7, 8, 9, 32)
 WS = (1,)
 WH = (0, 1, 3)
 NH = 7
@@ -38,6 +42,12 @@ ROWS_AT = (1, 5, 9, 13, 17, 21)
 NDUM = (3, 1, 0)
 LASTSPLIT = 2
 CV = ()
+XS = ()
+ELAG = 2
+VQ1 = "XVEt"
+VQ2 = "i"
+VQ3 = "vM"
+VQ4 = "xoq"
 FIN = True
 
 
@@ -74,24 +84,24 @@ def tile_attention_pa_t_kernel(tc, q, k, x, wv, mask, out):
 
         live = {}
 
-        def load_qk(b):
-            q_sb = raw.tile([P, H * S], BF16)
-            k_sb = raw.tile([P, H * S], BF16)
+        def load_qk(b, lo, hi):
+            if lo == 0:
+                q_sb = raw.tile([P, H * S], BF16)
+                k_sb = raw.tile([P, H * S], BF16)
+                live["q_sb", b], live["k_sb", b] = q_sb, k_sb
+            nc.sync.dma_start(
+                out=live["q_sb", b][:, lo * S : hi * S].rearrange("p (h f) -> p h f", f=S),
+                in_=q[b, lo:hi].rearrange("h (p a) c -> p h (a c)", a=CHUNKS),
+            )
+            nc.sync.dma_start(
+                out=live["k_sb", b][:, lo * S : hi * S].rearrange("p (f c) -> p f c", c=DH),
+                in_=k[b, lo:hi].rearrange("h (a p) c -> p (h a) c", p=P),
+            )
+
+        def load_mask(b):
             mask_sb = raw.tile([P, S], BF16)
-            for lo, hi in ((0, 1), (1, 2), (2, H)) if b == 0 else ((0, H),):
-                nc.sync.dma_start(
-                    out=q_sb[:, lo * S : hi * S].rearrange("p (h f) -> p h f", f=S),
-                    in_=q[b, lo:hi].rearrange("h (p a) c -> p h (a c)", a=CHUNKS),
-                )
-                nc.sync.dma_start(
-                    out=k_sb[:, lo * S : hi * S].rearrange("p (f c) -> p f c", c=DH),
-                    in_=k[b, lo:hi].rearrange("h (a p) c -> p (h a) c", p=P),
-                )
-                if lo == 0:
-                    nc.sync.dma_start(out=mask_sb[:], in_=mask[b].partition_broadcast(P))
-                    if b == 0:
-                        nc.sync.dma_start(out=mask_rows[0:B, :], in_=mask)
-            live["q_sb", b], live["k_sb", b], live["mask_sb", b] = q_sb, k_sb, mask_sb
+            nc.sync.dma_start(out=mask_sb[:], in_=mask[b].partition_broadcast(P))
+            live["mask_sb", b] = mask_sb
 
         def make_mask_term(b):
             mask_term = raw.tile([P, S], F32)
@@ -118,7 +128,11 @@ def tile_attention_pa_t_kernel(tc, q, k, x, wv, mask, out):
             x_sb = raw.tile([P, CHUNKS * D], BF16)
             slabs = x_sb[:].rearrange("p (j d) -> p j d", j=CHUNKS)
             if b < 0:
-                nc.sync.dma_start(out=slabs, in_=wv.rearrange("h c d -> c h d"))
+                for pair in range(2):
+                    nc.sync.dma_start(
+                        out=slabs[:, 2 * pair : 2 * pair + 2, :],
+                        in_=wv[2 * pair : 2 * pair + 2].rearrange("h c d -> c h d"),
+                    )
             else:
                 rows = x[:, b, :].rearrange("(u p e) d -> u p e d", u=2, e=2)
                 for u in range(2):
@@ -399,8 +413,7 @@ def tile_attention_pa_t_kernel(tc, q, k, x, wv, mask, out):
                 turn += 1
             return plan
 
-        x_plan = spread(0, XW + 1, XD)
-        x_plan[XW] = [-4, -3, -2, -1]
+        x_plan = spread(0, X0, XD)
         v_plan = spread(0, P0, DP)
         o_plan = spread(0, A0, DA)
 
@@ -433,16 +446,20 @@ def tile_attention_pa_t_kernel(tc, q, k, x, wv, mask, out):
                 transpose_x(slot, j)
             regroup_x(copy, slot)
 
+        moved = []
+
         def vector_work(n, order):
             for piece in order:
                 if piece == "X":
-                    for slot in slots(n - 1):
+                    for slot in ([-3, -1] if n == 2 else []) + slots(n - 1):
                         quantise_x(slot)
                 if piece == "V":
                     for m in projects(n - 1):
                         quantise_v(m)
-                if piece == "E" and is_step(n - EXP_LAG - 1):
-                    quantise_e(n - EXP_LAG - 1, 0, CHUNKS)
+                if piece == "E" and is_step(n - 2 - ELAG):
+                    quantise_e(n - 2 - ELAG, 0, CHUNKS)
+                if piece == "F" and ELAG == 2:
+                    quantise_e(n - 3, 0, CHUNKS)
                 if piece == "v":
                     for m in projects(n):
                         regroup_v(nc.vector.tensor_copy, m)
@@ -455,9 +472,10 @@ def tile_attention_pa_t_kernel(tc, q, k, x, wv, mask, out):
                     row_max(n - 1, 1, 3)
                 if piece == "M" and is_step(n - 1):
                     row_max(n - 1, 0, 3)
-                if piece == "x" and n != XW:
-                    for slot in slots(n)[:1]:
-                        regroup_x(nc.vector.tensor_copy, slot)
+                if piece == "x" and n > 1:
+                    for slot in [s for s in slots(n)[:1] if s not in moved]:
+                        moved.append(slot)
+                        regroup_x(nc.scalar.copy if slot >= 0 and slot % 16 in XS else nc.vector.tensor_copy, slot)
                 if piece == "t" and is_step(n - 2):
                     row_max_turned(n - 2)
                 if piece == "o":
@@ -472,10 +490,20 @@ def tile_attention_pa_t_kernel(tc, q, k, x, wv, mask, out):
                 nc.tensor.matmul(bank[:], lhsT=zeros[:, 0:P], rhs=zeros[:], start=True, stop=True)
 
         stack.enter_context(tc.manual_schedule())
-        load_qk(0)
-        load_rows(-1)
+        load_qk(0, 0, 1)
+        load_mask(0)
+        nc.sync.dma_start(out=mask_rows[0:B, :], in_=mask)
+        if WEARLY:
+            load_rows(-1)
+            load_qk(0, 1, 2)
+            load_qk(0, 2, H)
+        else:
+            load_qk(0, 1, 2)
+            load_qk(0, 2, H)
+            load_rows(-1)
         load_rows(0)
-        load_qk(1)
+        load_qk(1, 0, H)
+        load_mask(1)
         load_rows(1)
         dummy(NDUM[0])
         for j in range(CHUNKS):
@@ -483,29 +511,34 @@ def tile_attention_pa_t_kernel(tc, q, k, x, wv, mask, out):
         copy_qk(nc.scalar.copy, 0)
         dummy(NDUM[1])
         make_mask_term(0)
+        if WEARLY:
+            for slot in (-4, -2)[:WE]:
+                move_x(nc.vector.tensor_copy, slot)
         scores(0, 0)
         scores(0, 1)
         for j in range(CHUNKS):
             transpose_qk(1, j)
+        copy_qk(nc.vector.tensor_copy, 1)
         make_mask_cols()
         for n in range(STEPS + EXP_LAG):
             if (n + 2 + DMA_LEAD) % H == 0 and 2 * H <= n + 2 + DMA_LEAD < STEPS:
-                load_qk((n + 2 + DMA_LEAD) // H)
+                load_qk((n + 2 + DMA_LEAD) // H, 0, H)
+                load_mask((n + 2 + DMA_LEAD) // H)
             if n in ROWS_AT:
                 load_rows(2 + ROWS_AT.index(n))
             if is_step(n):
                 squash(n, 0)
                 if n == 0:
-                    add_mask(nc.vector, n, 0, 1)
+                    add_mask(nc.gpsimd if G0 else nc.vector, n, 0, 1)
             scores_ahead(n, 0)
-            if n == 0:
-                copy_qk(nc.vector.tensor_copy, 1)
+            if 2 < n < STEPS:
+                turn_back(n - 2)
             if n == STEPS:
                 turn_back(n - 1)
             if n == 1:
                 vector_work(n, "012")
             elif 2 < n < STEPS:
-                vector_work(n, "XV")
+                vector_work(n, VQ1)
             if n == 2:
                 for j in range(CHUNKS):
                     transpose_qk(3, j)
@@ -517,49 +550,52 @@ def tile_attention_pa_t_kernel(tc, q, k, x, wv, mask, out):
                 for m in projects(n):
                     for j in range(CHUNKS):
                         project_v(m, j)
-            if n > XW:
-                for slot in slots(n)[:1]:
-                    for j in range(CHUNKS):
-                        transpose_x(slot, j)
             exp_chunk(n - EXP_LAG, 0)
             if is_step(n - EXP_LAG - 1):
                 regroup_e(nc.vector.tensor_copy if n in CV else nc.scalar.copy, n - EXP_LAG - 1, 1)
+            vector_work(n, "" if n == 1 else "0" if n == 2 else "VEFi" if n == STEPS else ("F" if ELAG == 2 else "E") + "i" if n > STEPS else VQ2)
             if is_step(n):
                 squash(n, 1)
                 if n == STEPS - 1:
                     add_mask(nc.gpsimd, n, 0, LASTSPLIT)
                 if n == 0:
-                    add_mask(nc.vector, n, 1, 2)
+                    add_mask(nc.gpsimd if G0 else nc.vector, n, 1, 2)
             scores_ahead(n, 1)
-            if 2 < n < STEPS:
-                turn_back(n - 2)
+            if n > 1:
+                for slot in slots(n)[:1]:
+                    for j in range(CHUNKS):
+                        transpose_x(slot, j)
             exp_chunk(n - EXP_LAG, 1)
-            vector_work(n, "" if n == 1 else "0" if n == 2 else "VEvi" if n == STEPS else "Ei" if n > STEPS else "Evi0t")
+            vector_work(n, "x" if n <= 2 or n >= STEPS else VQ3)
             if is_step(n):
                 squash(n, 2)
                 if n == 0:
-                    add_mask(nc.vector, n, 2, 3)
+                    add_mask(nc.gpsimd if G0 else nc.vector, n, 2, 3)
                 elif n < STEPS - 1:
                     add_mask(nc.gpsimd, n, 0, TURNED)
             scores_ahead(n, 2)
-            if n == XW:
+            if n == 0 and WEARLY:
+                for slot in (-4, -2, -3, -1)[WE:WL]:
+                    move_x(nc.vector.tensor_copy, slot)
+            if n == 1:
                 turn_back(0)
                 row_max_turned(0)
-                for slot in slots(n)[:3]:
+                for slot in (-4, -2, -3, -1)[WL if WEARLY else 0:][:3]:
                     move_x(nc.vector.tensor_copy, slot)
             else:
-                vector_work(n, "x")
+                if len(slots(n)) > 1:
+                    vector_work(n, "x")
                 for slot in slots(n)[1:]:
-                    move_x(nc.vector.tensor_copy, slot)
+                    move_x(nc.scalar.copy if slot % 16 in XS else nc.vector.tensor_copy, slot)
             if n < STEPS:
                 for m in attends(n):
                     for j in range(CHUNKS):
                         attend(m, j)
-            if is_step(n + 2) and n != XW:
+            if is_step(n + 2) and n != 1:
                 for j in range(CHUNKS):
                     transpose_qk(n + 2, j)
             exp_chunk(n - EXP_LAG, 2)
-            vector_work(n, "" if n == XW or n >= STEPS else "qmX" if n == 2 else "oqm")
+            vector_work(n, "" if n == 1 or n >= STEPS else "qmX" if n == 2 else "q" if n == 0 else VQ4)
             if n == STEPS - 1:
                 if LASTSPLIT < 3:
                     add_mask(nc.vector, n, LASTSPLIT, 3)
@@ -569,8 +605,10 @@ def tile_attention_pa_t_kernel(tc, q, k, x, wv, mask, out):
             if is_step(n):
                 squash(n, 3)
             scores_ahead(n, 3)
-            if n == XW:
-                for slot in slots(n)[3:]:
+            if n == 1:
+                for slot in (-4, -2, -3, -1)[WL if WEARLY else 0:][3:]:
+                    move_x(nc.vector.tensor_copy, slot)
+                for slot in slots(n):
                     move_x(nc.vector.tensor_copy, slot)
             if n == STEPS - 1:
                 turn_back(n - 1)

@@ -39,9 +39,16 @@ WS = (1,)
 WH = (0, 1, 3)
 NH = 7
 ROWS_AT = (1, 5, 9, 13, 17, 21)
-NDUM = (3, 1, 0)
+NDUM = (3, 3, 0)
 LASTSPLIT = 2
 CV = ()
+TM = 1
+W3 = 3
+EX = True
+PAIRS = True
+VPAIRS = True
+MG = True
+MQ = 2
 XS = ()
 ELAG = 2
 VQ1 = "XVEt"
@@ -105,7 +112,7 @@ def tile_attention_pa_t_kernel(tc, q, k, x, wv, mask, out):
 
         def make_mask_term(b):
             mask_term = raw.tile([P, S], F32)
-            nc.vector.tensor_scalar(
+            (nc.gpsimd if MG and b else nc.vector).tensor_scalar(
                 out=mask_term[:], in0=live["mask_sb", b][:], scalar1=10000.0, scalar2=-10000.0, op0=ALU.mult, op1=ALU.add
             )
             live["mask_term", b] = mask_term
@@ -212,18 +219,25 @@ def tile_attention_pa_t_kernel(tc, q, k, x, wv, mask, out):
                 )
 
         def regroup_v(copy, n):
-            v_grouped = val.tile([P, 4 * DH], BF16, align_bytes=64)
+            if n % 2 == 0 or not VPAIRS:
+                v_grouped = val.tile([P, (2 if VPAIRS else 1) * 4 * DH], BF16, align_bytes=64)
+                live["v_grouped", n // 2 if VPAIRS else n] = v_grouped
+            off = n % 2 * 4 * DH if VPAIRS else 0
             copy(
-                out=v_grouped[:].rearrange("p (c j) -> p c j", j=4),
+                out=live["v_grouped", n // 2 if VPAIRS else n][:, off : off + 4 * DH].rearrange("p (c j) -> p c j", j=4),
                 in_=live["v_ps", n][:].rearrange("p (j c) -> p c j", j=4),
             )
-            live["v_grouped", n] = v_grouped
 
         def quantise_v(n):
-            v_codes = val.tile([P, DH], U32, align_bytes=64)
-            v_scales = val.tile([P, DH], U8, align_bytes=64)
-            nc.vector.quantize_mx(out=v_codes[:].bitcast(FP8X4), scales=v_scales[:], in_=live["v_grouped", n][:])
-            live["v_codes", n], live["v_scales", n] = v_codes, v_scales
+            if VPAIRS and n % 2 == 0:
+                return
+            w = 2 if VPAIRS else 1
+            v_codes = val.tile([P, w * DH], U32, align_bytes=64)
+            v_scales = val.tile([P, w * DH], U8, align_bytes=64)
+            nc.vector.quantize_mx(out=v_codes[:].bitcast(FP8X4), scales=v_scales[:], in_=live["v_grouped", n // 2 if VPAIRS else n][:])
+            for i in range(w):
+                cols = slice(i * DH, (i + 1) * DH)
+                live["v_codes", n - w + 1 + i], live["v_scales", n - w + 1 + i] = v_codes[:, cols], v_scales[:, cols]
 
         def transpose_qk(n, a):
             b, h = divmod(n, H)
@@ -238,7 +252,7 @@ def tile_attention_pa_t_kernel(tc, q, k, x, wv, mask, out):
                 )
 
         def copy_qk(copy, n):
-            qk_t = qk_pool.tile([P, 2 * S], BF16)
+            qk_t = qk_pool.tile([P, 2 * S], BF16, tag="qk_t")
             copy(out=qk_t[:], in_=live["qkt", n][:])
             live["qk_t", n] = qk_t
 
@@ -319,18 +333,23 @@ def tile_attention_pa_t_kernel(tc, q, k, x, wv, mask, out):
                 negate=True,
             )
 
+        def col(n):
+            return n % 2 * CHUNKS if PAIRS else 0
+
         def exponential(n, a):
             if a == 0:
                 e_sb = soft.tile([P, CHUNKS * S], BF16)
-                row_sum = kept.tile([P, CHUNKS], F32)
-                live["e_sb", n], live["row_sum", n] = e_sb, row_sum
+                live["e_sb", n] = e_sb
+                if n % 2 == 0 or not PAIRS:
+                    row_sum = kept.tile([P, 2 * CHUNKS], F32)
+                    live["row_sum", n // 2 if PAIRS else n] = row_sum
             nc.scalar.activation(
                 out=live["e_sb", n][:, a * S : (a + 1) * S],
                 in_=live["a_ps", n][:] if a == TURNED else live["att", n][:, a * S : (a + 1) * S],
                 func=ACT.Exp,
                 bias=live["neg_max", n][:, a : a + 1],
                 scale=1.0,
-                accum_out=live["row_sum", n][:, a : a + 1],
+                accum_out=live["row_sum", n // 2 if PAIRS else n][:, col(n) + a : col(n) + a + 1],
             )
 
         def transpose_e(n, a):
@@ -356,6 +375,14 @@ def tile_attention_pa_t_kernel(tc, q, k, x, wv, mask, out):
                 in_=live["et", n, pair][:].rearrange("p (u c) -> p c u", u=2),
             )
 
+        def regroup_e_chunk(copy, n, a):
+            pair, s = divmod(a, 2)
+            words = live["e_grouped", n][:].bitcast(F32).rearrange("p (c u) -> p c u", u=2)
+            copy(
+                out=words[:, a * P : (a + 1) * P, :],
+                in_=live["et", n, pair][:].rearrange("p (u i c) -> p i c u", u=2, i=2)[:, s],
+            )
+
         def quantise_e(n, lo, hi):
             if lo == 0:
                 e_codes = kept.tile([P, S], U32, align_bytes=64)
@@ -377,16 +404,27 @@ def tile_attention_pa_t_kernel(tc, q, k, x, wv, mask, out):
                 out=live["o_ps", n][:, a * DH : (a + 1) * DH],
                 lhsT=live["e_codes", n][:, cols].bitcast(FP8X4),
                 lhsT_scale=live["e_scales", n][:, cols],
-                rhs=live["v_codes", n][:].bitcast(FP8X4),
-                rhs_scale=live["v_scales", n][:],
+                rhs=live["v_codes", n].bitcast(FP8X4),
+                rhs_scale=live["v_scales", n],
                 start=True,
                 stop=True,
             )
 
         def invert_row_sum(n):
-            inv_sum = kept.tile([P, CHUNKS], F32)
-            nc.vector.reciprocal(out=inv_sum[:], in_=live["row_sum", n][:])
-            live["inv_sum", n] = inv_sum
+            if PAIRS:
+                if n % 2 == 0:
+                    inv_sum = kept.tile([P, 2 * CHUNKS], F32)
+                    live["inv_sum", n // 2] = inv_sum
+                if n < STEPS - 2:
+                    cols = slice(0, 2 * CHUNKS) if n % 2 == 0 else slice(0, 0)
+                else:
+                    cols = slice(col(n), col(n) + CHUNKS)
+                if n % 2 == 0 or n == STEPS - 1:
+                    nc.vector.reciprocal(out=live["inv_sum", n // 2][:, cols], in_=live["row_sum", n // 2][:, cols])
+            else:
+                inv_sum = kept.tile([P, CHUNKS], F32)
+                nc.vector.reciprocal(out=inv_sum[:], in_=live["row_sum", n][:, 0:CHUNKS])
+                live["inv_sum", n] = inv_sum
 
         def normalise_and_store(n, lo, hi):
             b, h = divmod(n, H)
@@ -395,7 +433,7 @@ def tile_attention_pa_t_kernel(tc, q, k, x, wv, mask, out):
             nc.vector.tensor_tensor(
                 out=o_view,
                 in0=live["o_ps", n][:, lo * DH : hi * DH].rearrange("p (a c) -> p a c", c=DH),
-                in1=live["inv_sum", n][:, lo:hi].unsqueeze(2).to_broadcast([P, hi - lo, DH]),
+                in1=live["inv_sum", n // 2 if PAIRS else n][:, col(n) + lo : col(n) + hi].unsqueeze(2).to_broadcast([P, hi - lo, DH]),
                 op=ALU.mult,
             )
             rows = out[:, b, h * DH : (h + 1) * DH].rearrange("(p a) c -> p a c", a=CHUNKS)
@@ -506,9 +544,13 @@ def tile_attention_pa_t_kernel(tc, q, k, x, wv, mask, out):
         load_mask(1)
         load_rows(1)
         dummy(NDUM[0])
-        for j in range(CHUNKS):
-            transpose_qk(0, j)
-        copy_qk(nc.scalar.copy, 0)
+        qk_t = qk_pool.tile([P, 2 * S], BF16, tag="qk_t")
+        live["qk_t", 0] = qk_t
+        for which, rows_sb, copy in ((0, live["q_sb", 0], nc.vector.tensor_copy), (1, live["k_sb", 0], nc.scalar.copy)):
+            half_qkt = ps_two.tile([P, S], BF16, tag="w")
+            for j in range(CHUNKS):
+                nc.tensor.transpose(half_qkt[:, j * P : (j + 1) * P], rows_sb[:, j * DH : (j + 1) * DH], ident_bf[:])
+            copy(out=qk_t[:, which * S : (which + 1) * S], in_=half_qkt[:])
         dummy(NDUM[1])
         make_mask_term(0)
         if WEARLY:
@@ -561,12 +603,19 @@ def tile_attention_pa_t_kernel(tc, q, k, x, wv, mask, out):
                 if n == 0:
                     add_mask(nc.gpsimd if G0 else nc.vector, n, 1, 2)
             scores_ahead(n, 1)
+            if EX:
+                exp_chunk(n - EXP_LAG, 1)
             if n > 1:
                 for slot in slots(n)[:1]:
                     for j in range(CHUNKS):
                         transpose_x(slot, j)
-            exp_chunk(n - EXP_LAG, 1)
+            if not EX:
+                exp_chunk(n - EXP_LAG, 1)
             vector_work(n, "x" if n <= 2 or n >= STEPS else VQ3)
+            if n > STEPS:
+                for m in attends(n - 1):
+                    for j in range(CHUNKS):
+                        attend(m, j)
             if is_step(n):
                 squash(n, 2)
                 if n == 0:
@@ -580,7 +629,7 @@ def tile_attention_pa_t_kernel(tc, q, k, x, wv, mask, out):
             if n == 1:
                 turn_back(0)
                 row_max_turned(0)
-                for slot in (-4, -2, -3, -1)[WL if WEARLY else 0:][:3]:
+                for slot in (-4, -2, -3, -1)[WL if WEARLY else 0:][:W3]:
                     move_x(nc.vector.tensor_copy, slot)
             else:
                 if len(slots(n)) > 1:
@@ -600,38 +649,48 @@ def tile_attention_pa_t_kernel(tc, q, k, x, wv, mask, out):
                 if LASTSPLIT < 3:
                     add_mask(nc.vector, n, LASTSPLIT, 3)
                 row_max(n, 0, 1)
-            if 0 <= n - EXP_LAG < STEPS - 1:
+            if 0 <= n - EXP_LAG:
                 regroup_e(nc.scalar.copy, n - EXP_LAG, 0)
             if is_step(n):
                 squash(n, 3)
             scores_ahead(n, 3)
             if n == 1:
-                for slot in (-4, -2, -3, -1)[WL if WEARLY else 0:][3:]:
+                for slot in (-4, -2, -3, -1)[WL if WEARLY else 0:][W3:]:
                     move_x(nc.vector.tensor_copy, slot)
                 for slot in slots(n):
                     move_x(nc.vector.tensor_copy, slot)
             if n == STEPS - 1:
                 turn_back(n - 1)
                 row_max_turned(n - 1)
-            if is_step(n + 1) and (n + 1) % H == 0:
+            if not MG and is_step(n + 1) and (n + 1) % H == 0:
                 make_mask_term((n + 1) // H)
+            if MG and n % H == MQ and n // H + 1 < B:
+                make_mask_term(n // H + 1)
             exp_chunk(n - EXP_LAG, 3)
-            if n >= STEPS:
-                for m in attends(n):
-                    for j in range(CHUNKS):
-                        attend(m, j)
-                vector_work(n, "o")
 
         last = STEPS - 1
         half = CHUNKS // 2
-        regroup_e(nc.scalar.copy if FIN else nc.vector.tensor_copy, last, 0)
         regroup_e(nc.scalar.copy, last, 1)
         quantise_e(last, 0, half)
-        for a in range(half):
-            attend(last, a)
-        invert_row_sum(last)
-        normalise_and_store(last, 0, half)
-        quantise_e(last, half, CHUNKS)
-        for a in range(half, CHUNKS):
-            attend(last, a)
-        normalise_and_store(last, half, CHUNKS)
+        for m in attends(STEPS + 1):
+            for j in range(CHUNKS):
+                attend(m, j)
+        if TM == 0:
+            for a in range(half):
+                attend(last, a)
+        vector_work(STEPS, "o")
+        if TM == 1:
+            quantise_e(last, half, CHUNKS)
+            for a in range(CHUNKS):
+                attend(last, a)
+            invert_row_sum(last)
+            vector_work(STEPS + 1, "o")
+            normalise_and_store(last, 0, CHUNKS)
+        else:
+            invert_row_sum(last)
+            vector_work(STEPS + 1, "o")
+            normalise_and_store(last, 0, half)
+            quantise_e(last, half, CHUNKS)
+            for a in range(half, CHUNKS):
+                attend(last, a)
+            normalise_and_store(last, half, CHUNKS)

@@ -26,15 +26,15 @@ TURNED = 3
 DMA_LEAD = 4
 SOFT = 5
 X0 = 2
-XD = (2, 3, 4, 5, 6)
+XD = (2, 3, 4, 5)
 G0 = True
 WEARLY = False
 WE = 2
 WL = 3
 P0 = 5
-DP = (5, 6, 7, 30, 31)
+DP = (5, 6, 29, 30, 31)
 A0 = 7
-DA = (7, 8, 9, 32)
+DA = (30, 31, 32, 33)
 WS = (1,)
 WH = (0, 1, 3)
 NH = 7
@@ -42,6 +42,8 @@ ROWS_AT = (1, 5, 9, 13, 17, 21)
 NDUM = (3, 3, 0)
 LASTSPLIT = 2
 CV = ()
+DS = ((2, 1), (2, 3), (3, 1), (3, 3))
+TW = False
 TM = 1
 W3 = 3
 EX = True
@@ -261,6 +263,8 @@ def tile_attention_pa_t_kernel(tc, q, k, x, wv, mask, out):
             s_ps = ps_s.tile([P, S], F32, tag="s")
             if n > 3 and a in (WS if n >= NH else WH):
                 keep_warm(s_ps)
+            if (n, a) in DS:
+                nc.tensor.matmul(s_ps[:], lhsT=zeros[:, 0:P], rhs=zeros[:], start=True, stop=True)
             queries = qk_t[:, a * P : (a + 1) * P]
             if a == TURNED:
                 for j in range(CHUNKS):
@@ -477,6 +481,9 @@ def tile_attention_pa_t_kernel(tc, q, k, x, wv, mask, out):
         def exp_chunk(n, a):
             if is_step(n):
                 exponential(n, a)
+                if n >= STEPS - 2 and TW:
+                    bank = ps_a.tile([P, S], F32, tag="a")
+                    keep_warm(bank)
                 transpose_e(n, a)
 
         def move_x(copy, slot):

@@ -42,11 +42,14 @@ ROWS_AT = (1, 5, 9, 13, 17, 21)
 NDUM = (3, 3, 0)
 LASTSPLIT = 2
 CV = ()
+LATEV = False
+CV0 = (9, 13, 17, 21, 25)
 DS = ((2, 1), (2, 3), (3, 1), (3, 3))
 TW = False
-TM = 1
+FT = 2
+AT = 2
 W3 = 3
-EX = True
+CT = False
 PAIRS = True
 VPAIRS = True
 MG = True
@@ -595,11 +598,13 @@ def tile_attention_pa_t_kernel(tc, q, k, x, wv, mask, out):
             if n == STEPS:
                 vector_work(n, "m")
                 row_max_turned(n - 1)
-            if n < STEPS:
+            if n < STEPS and not (LATEV and not slots(n)):
                 for m in projects(n):
                     for j in range(CHUNKS):
                         project_v(m, j)
             exp_chunk(n - EXP_LAG, 0)
+            if n >= STEPS and CT:
+                exp_chunk(n - EXP_LAG, 1)
             if is_step(n - EXP_LAG - 1):
                 regroup_e(nc.vector.tensor_copy if n in CV else nc.scalar.copy, n - EXP_LAG - 1, 1)
             vector_work(n, "" if n == 1 else "0" if n == 2 else "VEFi" if n == STEPS else ("F" if ELAG == 2 else "E") + "i" if n > STEPS else VQ2)
@@ -610,17 +615,19 @@ def tile_attention_pa_t_kernel(tc, q, k, x, wv, mask, out):
                 if n == 0:
                     add_mask(nc.gpsimd if G0 else nc.vector, n, 1, 2)
             scores_ahead(n, 1)
-            if EX:
+            if not (n >= STEPS and CT):
                 exp_chunk(n - EXP_LAG, 1)
+            if n < STEPS and LATEV and not slots(n):
+                for m in projects(n):
+                    for j in range(CHUNKS):
+                        project_v(m, j)
             if n > 1:
                 for slot in slots(n)[:1]:
                     for j in range(CHUNKS):
                         transpose_x(slot, j)
-            if not EX:
-                exp_chunk(n - EXP_LAG, 1)
             vector_work(n, "x" if n <= 2 or n >= STEPS else VQ3)
             if n > STEPS:
-                for m in attends(n - 1):
+                for m in attends(n - 1)[:AT]:
                     for j in range(CHUNKS):
                         attend(m, j)
             if is_step(n):
@@ -651,12 +658,16 @@ def tile_attention_pa_t_kernel(tc, q, k, x, wv, mask, out):
                 for j in range(CHUNKS):
                     transpose_qk(n + 2, j)
             exp_chunk(n - EXP_LAG, 2)
+            if n in CV0:
+                regroup_e(nc.vector.tensor_copy, n - EXP_LAG, 0)
             vector_work(n, "" if n == 1 or n >= STEPS else "qmX" if n == 2 else "q" if n == 0 else VQ4)
             if n == STEPS - 1:
                 if LASTSPLIT < 3:
                     add_mask(nc.vector, n, LASTSPLIT, 3)
                 row_max(n, 0, 1)
-            if 0 <= n - EXP_LAG:
+            if n >= STEPS and CT:
+                exp_chunk(n - EXP_LAG, 3)
+            if 0 <= n - EXP_LAG and n not in CV0:
                 regroup_e(nc.scalar.copy, n - EXP_LAG, 0)
             if is_step(n):
                 squash(n, 3)
@@ -673,31 +684,34 @@ def tile_attention_pa_t_kernel(tc, q, k, x, wv, mask, out):
                 make_mask_term((n + 1) // H)
             if MG and n % H == MQ and n // H + 1 < B:
                 make_mask_term(n // H + 1)
-            exp_chunk(n - EXP_LAG, 3)
+            if not (n >= STEPS and CT):
+                exp_chunk(n - EXP_LAG, 3)
 
         last = STEPS - 1
         half = CHUNKS // 2
         regroup_e(nc.scalar.copy, last, 1)
         quantise_e(last, 0, half)
-        for m in attends(STEPS + 1):
+        for m in attends(STEPS)[AT:] + attends(STEPS + 1):
             for j in range(CHUNKS):
                 attend(m, j)
-        if TM == 0:
-            for a in range(half):
-                attend(last, a)
+        for a in range(half):
+            attend(last, a)
         vector_work(STEPS, "o")
-        if TM == 1:
-            quantise_e(last, half, CHUNKS)
-            for a in range(CHUNKS):
-                attend(last, a)
-            invert_row_sum(last)
-            vector_work(STEPS + 1, "o")
-            normalise_and_store(last, 0, CHUNKS)
-        else:
-            invert_row_sum(last)
+        invert_row_sum(last)
+        if FT == 0:
             vector_work(STEPS + 1, "o")
             normalise_and_store(last, 0, half)
             quantise_e(last, half, CHUNKS)
-            for a in range(half, CHUNKS):
-                attend(last, a)
-            normalise_and_store(last, half, CHUNKS)
+        if FT == 1:
+            quantise_e(last, half, CHUNKS)
+            vector_work(STEPS + 1, "o")
+        if FT == 2:
+            normalise_and_store(attends(STEPS + 1)[0], 0, CHUNKS)
+            normalise_and_store(last, 0, half)
+            quantise_e(last, half, CHUNKS)
+            normalise_and_store(attends(STEPS + 1)[1], 0, CHUNKS)
+        for a in range(half, CHUNKS):
+            attend(last, a)
+        if FT == 1:
+            normalise_and_store(last, 0, half)
+        normalise_and_store(last, half, CHUNKS)

from contextlib import ExitStack
import math

import concourse.mybir as mybir
from concourse.masks import make_identity

F32 = mybir.dt.float32
BF16 = mybir.dt.bfloat16
U32 = mybir.dt.uint32
U8 = mybir.dt.uint8
FP8X4 = mybir.dt.float8_e4m3fn_x4
ACT = mybir.ActivationFunctionType
ALU = mybir.AluOpType

S, B, D, H, DH = 512, 8, 1024, 4, 128
P = 128
CHUNKS = S // P
K_PASS = 512
PASSES = D // K_PASS
STEPS = B * H

FLOPS = 2 * S * B * D * H * DH + 2 * 2 * B * H * S * S * DH

EXP_LAG = 2
TURNED = 3
DMA_LEAD = 4
SOFT = 5
X0 = 2
XD = (2, 3, 4, 5)
G0 = True
WEARLY = False
WE = 2
WL = 3
P0 = 5
DP = (5, 6, 29, 30, 31)
A0 = 7
DA = (30, 31, 32, 33)
WS = (1,)
WH = (0, 1, 3)
NH = 7
ROWS_AT = (1, 5, 9, 13, 17, 21)
NDUM = (3, 3, 0)
LASTSPLIT = 2
CV = ()
LATEV = False
CV0 = (9, 13, 17, 21, 25)
DS = ((2, 1), (2, 3), (3, 1), (3, 3))
TW = False
FT = 2
AT = 2
W3 = 3
CT = False
PAIRS = True
VPAIRS = True
MG = True
MQ = 2
XS = ()
ELAG = 2
VQ1 = "XVEt"
VQ2 = "i"
VQ3 = "vM"
VQ4 = "xoq"
FIN = True


def tile_attention_pa_t_kernel(tc, q, k, x, wv, mask, out):
    nc = tc.nc
    with ExitStack() as stack:
        pool = lambda name, bufs: stack.enter_context(tc.tile_pool(name=name, bufs=bufs))
        psum = lambda name, bufs: stack.enter_context(tc.psum_pool(name=name, bufs=bufs))
        const = pool("const", 1)
        raw = pool("raw", 3)
        proj = pool("proj", 2)
        qk_pool = pool("qk", 4)
        soft = pool("soft", SOFT)
        kept = pool("kept", 10)
        val = pool("val", 4)
        res = pool("res", 6)
        ps_s = psum("ps_s", 2)
        ps_et = psum("ps_et", 2)
        ps_two = psum("ps_two", 3)
        ps_a = psum("ps_a", 1)

        ident_f32 = const.tile([P, P], F32)
        make_identity(nc, ident_f32[:])
        ident_bf = const.tile([P, P], BF16)
        make_identity(nc, ident_bf[:])
        w_codes = const.tile([P, PASSES * S], U32, align_bytes=64)
        w_scales = const.tile([P, PASSES * S], U8, align_bytes=64)

        zeros = const.tile([P, S], BF16)
        nc.vector.memset(zeros[:], 0.0)
        mask_rows = const.tile([P, S], BF16)
        nc.vector.memset(mask_rows[:], 0.0)
        mask_cols = const.tile([P, CHUNKS * B], F32)

        live = {}

        def load_qk(b, lo, hi):
            if lo == 0:
                q_sb = raw.tile([P, H * S], BF16)
                k_sb = raw.tile([P, H * S], BF16)
                live["q_sb", b], live["k_sb", b] = q_sb, k_sb
            nc.sync.dma_start(
                out=live["q_sb", b][:, lo * S : hi * S].rearrange("p (h f) -> p h f", f=S),
                in_=q[b, lo:hi].rearrange("h (p a) c -> p h (a c)", a=CHUNKS),
            )
            nc.sync.dma_start(
                out=live["k_sb", b][:, lo * S : hi * S].rearrange("p (f c) -> p f c", c=DH),
                in_=k[b, lo:hi].rearrange("h (a p) c -> p (h a) c", p=P),
            )

        def load_mask(b):
            mask_sb = raw.tile([P, S], BF16)
            nc.sync.dma_start(out=mask_sb[:], in_=mask[b].partition_broadcast(P))
            live["mask_sb", b] = mask_sb

        def make_mask_term(b):
            mask_term = raw.tile([P, S], F32)
            (nc.gpsimd if MG and b else nc.vector).tensor_scalar(
                out=mask_term[:], in0=live["mask_sb", b][:], scalar1=10000.0, scalar2=-10000.0, op0=ALU.mult, op1=ALU.add
            )
            live["mask_term", b] = mask_term

        def make_mask_cols():
            mt = ps_two.tile([P, CHUNKS * P], BF16, tag="w")
            for j in range(CHUNKS):
                cols = slice(j * P, (j + 1) * P)
                nc.tensor.transpose(mt[:, cols], mask_rows[:, cols], ident_bf[:])
            nc.vector.tensor_scalar(
                out=mask_cols[:].rearrange("p (j b) -> p j b", j=CHUNKS),
                in0=mt[:].rearrange("p (j r) -> p j r", j=CHUNKS)[:, :, 0:B],
                scalar1=10000.0,
                scalar2=-10000.0,
                op0=ALU.mult,
                op1=ALU.add,
            )

        def load_rows(b):
            x_sb = raw.tile([P, CHUNKS * D], BF16)
            slabs = x_sb[:].rearrange("p (j d) -> p j d", j=CHUNKS)
            if b < 0:
                for pair in range(2):
                    nc.sync.dma_start(
                        out=slabs[:, 2 * pair : 2 * pair + 2, :],
                        in_=wv[2 * pair : 2 * pair + 2].rearrange("h c d -> c h d"),
                    )
            else:
                rows = x[:, b, :].rearrange("(u p e) d -> u p e d", u=2, e=2)
                for u in range(2):
                    nc.sync.dma_start(out=slabs[:, 2 * u : 2 * u + 2, :], in_=rows[u])
            live["x_sb", b] = x_sb

        def transpose_x(slot, quarter):
            b, h = divmod(slot, H)
            g, pair = divmod(h, 2)
            u, s = divmod(quarter, 2)
            if quarter == 0:
                xt = ps_two.tile([P, 512], F32, tag="w")
                live["xt", slot] = xt
            first = (2 * pair + s) * (D // 2) + (2 * g + u) * P
            nc.tensor.transpose(
                live["xt", slot][:, quarter * P : (quarter + 1) * P],
                live["x_sb", b][:].bitcast(F32)[:, first : first + P],
                ident_f32[:],
            )

        def regroup_x(copy, slot):
            b, h = divmod(slot, H)
            g, pair = divmod(h, 2)
            if h == 0:
                x_grouped = proj.tile([P, PASSES * 4 * S], BF16, align_bytes=64)
                live["x_grouped", b] = x_grouped
                if b < 0:
                    live["x_codes", b], live["x_scales", b] = w_codes, w_scales
                else:
                    x_codes = proj.tile([P, PASSES * S], U32, align_bytes=64)
                    x_scales = proj.tile([P, PASSES * S], U8, align_bytes=64)
                    live["x_codes", b], live["x_scales", b] = x_codes, x_scales
            words = live["x_grouped", b][:].bitcast(F32).rearrange("p (g c u) -> p g c u", g=PASSES, u=2)
            copy(
                out=words[:, g, 256 * pair : 256 * (pair + 1), :],
                in_=live["xt", slot][:].rearrange("p (u c) -> p c u", u=2),
            )

        def quantise_x(slot):
            b, h = divmod(slot, H)
            g, pair = divmod(h, 2)
            if pair == 1:
                cols = slice(g * S, (g + 1) * S)
                nc.vector.quantize_mx(
                    out=live["x_codes", b][:, cols].bitcast(FP8X4),
                    scales=live["x_scales", b][:, cols],
                    in_=live["x_grouped", b][:, g * 4 * S : (g + 1) * 4 * S],
                )

        def keep_warm(bank):
            nc.tensor.matmul_mx(
                out=bank[:],
                lhsT=w_codes[:, 0:P].bitcast(FP8X4),
                lhsT_scale=w_scales[:, 0:P],
                rhs=w_codes[:, 0:S].bitcast(FP8X4),
                rhs_scale=w_scales[:, 0:S],
                start=True,
                stop=True,
            )

        def project_v(n, j):
            b, h = divmod(n, H)
            if j == 0:
                v_ps = ps_two.tile([P, CHUNKS * DH], F32, tag="w")
                live["v_ps", n] = v_ps
            for g in range(PASSES):
                rows = slice(g * S + j * P, g * S + (j + 1) * P)
                cols = slice(g * S + h * DH, g * S + (h + 1) * DH)
                nc.tensor.matmul_mx(
                    out=live["v_ps", n][:, j * DH : (j + 1) * DH],
                    lhsT=live["x_codes", b][:, rows].bitcast(FP8X4),
                    lhsT_scale=live["x_scales", b][:, rows],
                    rhs=w_codes[:, cols].bitcast(FP8X4),
                    rhs_scale=w_scales[:, cols],
                    start=(g == 0),
                    stop=(g == PASSES - 1),
                )

        def regroup_v(copy, n):
            if n % 2 == 0 or not VPAIRS:
                v_grouped = val.tile([P, (2 if VPAIRS else 1) * 4 * DH], BF16, align_bytes=64)
                live["v_grouped", n // 2 if VPAIRS else n] = v_grouped
            off = n % 2 * 4 * DH if VPAIRS else 0
            copy(
                out=live["v_grouped", n // 2 if VPAIRS else n][:, off : off + 4 * DH].rearrange("p (c j) -> p c j", j=4),
                in_=live["v_ps", n][:].rearrange("p (j c) -> p c j", j=4),
            )

        def quantise_v(n):
            if VPAIRS and n % 2 == 0:
                return
            w = 2 if VPAIRS else 1
            v_codes = val.tile([P, w * DH], U32, align_bytes=64)
            v_scales = val.tile([P, w * DH], U8, align_bytes=64)
            nc.vector.quantize_mx(out=v_codes[:].bitcast(FP8X4), scales=v_scales[:], in_=live["v_grouped", n // 2 if VPAIRS else n][:])
            for i in range(w):
                cols = slice(i * DH, (i + 1) * DH)
                live["v_codes", n - w + 1 + i], live["v_scales", n - w + 1 + i] = v_codes[:, cols], v_scales[:, cols]

        def transpose_qk(n, a):
            b, h = divmod(n, H)
            if a == 0:
                qkt = ps_two.tile([P, 2 * S], BF16, tag="w")
                live["qkt", n] = qkt
            for which, rows_sb in enumerate((live["q_sb", b], live["k_sb", b])):
                nc.tensor.transpose(
                    live["qkt", n][:, which * S + a * P : which * S + (a + 1) * P],
                    rows_sb[:, (h * CHUNKS + a) * DH : (h * CHUNKS + a + 1) * DH],
                    ident_bf[:],
                )

        def copy_qk(copy, n):
            qk_t = qk_pool.tile([P, 2 * S], BF16, tag="qk_t")
            copy(out=qk_t[:], in_=live["qkt", n][:])
            live["qk_t", n] = qk_t

        def scores(n, a):
            qk_t = live["qk_t", n]
            s_ps = ps_s.tile([P, S], F32, tag="s")
            if n > 3 and a in (WS if n >= NH else WH):
                keep_warm(s_ps)
            if (n, a) in DS:
                nc.tensor.matmul(s_ps[:], lhsT=zeros[:, 0:P], rhs=zeros[:], start=True, stop=True)
            queries = qk_t[:, a * P : (a + 1) * P]
            if a == TURNED:
                for j in range(CHUNKS):
                    keys = qk_t[:, S + j * P : S + (j + 1) * P]
                    nc.tensor.matmul(s_ps[:, j * P : (j + 1) * P], lhsT=keys, rhs=queries, start=True, stop=True)
            else:
                nc.tensor.matmul(s_ps[:], lhsT=queries, rhs=qk_t[:, S : 2 * S], start=True, stop=True)
            live["s_ps", n, a] = s_ps

        def squash(n, a):
            if a == 0:
                att = soft.tile([P, CHUNKS * S], F32)
                live["att", n] = att
            nc.scalar.activation(
                out=live["att", n][:, a * S : (a + 1) * S],
                in_=live["s_ps", n, a][:],
                func=ACT.Tanh,
                scale=1.0 / math.sqrt(DH),
            )

        def add_mask(engine, n, lo, hi):
            chunks = live["att", n][:, lo * S : hi * S].rearrange("p (a t) -> p a t", a=hi - lo)
            term = live["mask_term", n // H][:].unsqueeze(1).to_broadcast([P, hi - lo, S])
            engine.tensor_tensor(out=chunks, in0=chunks, in1=term, op=ALU.add)

        def turn_back(n):
            if n < STEPS - 2:
                a_ps = ps_a.tile([P, S], F32, tag="a")
            else:
                a_ps = ps_s.tile([P, S], F32, tag="s")
            for j in range(CHUNKS):
                cols = slice(j * P, (j + 1) * P)
                first = TURNED * S + j * P
                nc.tensor.matmul(
                    a_ps[:, cols],
                    lhsT=live["att", n][:, first : first + P],
                    rhs=ident_f32[:],
                    start=True,
                    stop=False,
                    is_transpose=True,
                )
                nc.tensor.matmul(
                    a_ps[:, cols],
                    lhsT=mask_cols[:, j * B + n // H : j * B + n // H + 1].to_broadcast([P, P]),
                    rhs=ident_f32[:],
                    start=False,
                    stop=True,
                    is_transpose=True,
                )
            live["a_ps", n] = a_ps

        def row_max(n, lo=0, hi=TURNED):
            if lo == 0:
                neg_max = soft.tile([P, CHUNKS], F32)
                live["neg_max", n] = neg_max
            nc.vector.tensor_reduce(
                out=live["neg_max", n][:, lo:hi],
                in_=live["att", n][:, lo * S : hi * S].rearrange("p (a t) -> p a t", a=hi - lo),
                axis=mybir.AxisListType.X,
                op=ALU.max,
                negate=True,
            )

        def row_max_turned(n):
            nc.vector.tensor_reduce(
                out=live["neg_max", n][:, TURNED : TURNED + 1],
                in_=live["a_ps", n][:],
                axis=mybir.AxisListType.X,
                op=ALU.max,
                negate=True,
            )

        def col(n):
            return n % 2 * CHUNKS if PAIRS else 0

        def exponential(n, a):
            if a == 0:
                e_sb = soft.tile([P, CHUNKS * S], BF16)
                live["e_sb", n] = e_sb
                if n % 2 == 0 or not PAIRS:
                    row_sum = kept.tile([P, 2 * CHUNKS], F32)
                    live["row_sum", n // 2 if PAIRS else n] = row_sum
            nc.scalar.activation(
                out=live["e_sb", n][:, a * S : (a + 1) * S],
                in_=live["a_ps", n][:] if a == TURNED else live["att", n][:, a * S : (a + 1) * S],
                func=ACT.Exp,
                bias=live["neg_max", n][:, a : a + 1],
                scale=1.0,
                accum_out=live["row_sum", n // 2 if PAIRS else n][:, col(n) + a : col(n) + a + 1],
            )

        def transpose_e(n, a):
            pair, s = divmod(a, 2)
            if s == 0:
                et = ps_et.tile([P, 512], F32)
                live["et", n, pair] = et
            for u in range(2):
                first = a * (S // 2) + u * P
                nc.tensor.transpose(
                    live["et", n, pair][:, (2 * u + s) * P : (2 * u + s + 1) * P],
                    live["e_sb", n][:].bitcast(F32)[:, first : first + P],
                    ident_f32[:],
                )

        def regroup_e(copy, n, pair):
            if pair == 0:
                e_grouped = soft.tile([P, 4 * S], BF16, align_bytes=64)
                live["e_grouped", n] = e_grouped
            words = live["e_grouped", n][:].bitcast(F32).rearrange("p (c u) -> p c u", u=2)
            copy(
                out=words[:, 256 * pair : 256 * (pair + 1), :],
                in_=live["et", n, pair][:].rearrange("p (u c) -> p c u", u=2),
            )

        def regroup_e_chunk(copy, n, a):
            pair, s = divmod(a, 2)
            words = live["e_grouped", n][:].bitcast(F32).rearrange("p (c u) -> p c u", u=2)
            copy(
                out=words[:, a * P : (a + 1) * P, :],
                in_=live["et", n, pair][:].rearrange("p (u i c) -> p i c u", u=2, i=2)[:, s],
            )

        def quantise_e(n, lo, hi):
            if lo == 0:
                e_codes = kept.tile([P, S], U32, align_bytes=64)
                e_scales = kept.tile([P, S], U8, align_bytes=64)
                live["e_codes", n], live["e_scales", n] = e_codes, e_scales
            cols = slice(lo * P, hi * P)
            nc.vector.quantize_mx(
                out=live["e_codes", n][:, cols].bitcast(FP8X4),
                scales=live["e_scales", n][:, cols],
                in_=live["e_grouped", n][:, lo * S : hi * S],
            )

        def attend(n, a):
            if a == 0:
                o_ps = ps_two.tile([P, CHUNKS * DH], F32, tag="w")
                live["o_ps", n] = o_ps
            cols = slice(a * P, (a + 1) * P)
            nc.tensor.matmul_mx(
                out=live["o_ps", n][:, a * DH : (a + 1) * DH],
                lhsT=live["e_codes", n][:, cols].bitcast(FP8X4),
                lhsT_scale=live["e_scales", n][:, cols],
                rhs=live["v_codes", n].bitcast(FP8X4),
                rhs_scale=live["v_scales", n],
                start=True,
                stop=True,
            )

        def invert_row_sum(n):
            if PAIRS:
                if n % 2 == 0:
                    inv_sum = kept.tile([P, 2 * CHUNKS], F32)
                    live["inv_sum", n // 2] = inv_sum
                if n < STEPS - 2:
                    cols = slice(0, 2 * CHUNKS) if n % 2 == 0 else slice(0, 0)
                else:
                    cols = slice(col(n), col(n) + CHUNKS)
                if n % 2 == 0 or n == STEPS - 1:
                    nc.vector.reciprocal(out=live["inv_sum", n // 2][:, cols], in_=live["row_sum", n // 2][:, cols])
            else:
                inv_sum = kept.tile([P, CHUNKS], F32)
                nc.vector.reciprocal(out=inv_sum[:], in_=live["row_sum", n][:, 0:CHUNKS])
                live["inv_sum", n] = inv_sum

        def normalise_and_store(n, lo, hi):
            b, h = divmod(n, H)
            o_sb = res.tile([P, (hi - lo) * DH], F32, tag="o_sb")
            o_view = o_sb[:].rearrange("p (a c) -> p a c", c=DH)
            nc.vector.tensor_tensor(
                out=o_view,
                in0=live["o_ps", n][:, lo * DH : hi * DH].rearrange("p (a c) -> p a c", c=DH),
                in1=live["inv_sum", n // 2 if PAIRS else n][:, col(n) + lo : col(n) + hi].unsqueeze(2).to_broadcast([P, hi - lo, DH]),
                op=ALU.mult,
            )
            rows = out[:, b, h * DH : (h + 1) * DH].rearrange("(p a) c -> p a c", a=CHUNKS)
            nc.sync.dma_start(out=rows[:, lo:hi, :], in_=o_view)

        def is_step(n):
            return 0 <= n < STEPS

        def spread(first, turn, doubles):
            plan, item = {}, first
            while item < STEPS:
                count = 2 if turn in doubles else 1
                plan[turn] = [i for i in range(item, item + count) if i < STEPS]
                item += count
                turn += 1
            return plan

        x_plan = spread(0, X0, XD)
        v_plan = spread(0, P0, DP)
        o_plan = spread(0, A0, DA)

        def slots(n):
            return x_plan.get(n, [])

        def projects(n):
            return v_plan.get(n, [])

        def attends(n):
            return o_plan.get(n, [])

        def prepare_qk(n, copy):
            for j in range(CHUNKS):
                transpose_qk(n, j)
            copy_qk(copy, n)

        def scores_ahead(n, a):
            n, a = divmod(n * CHUNKS + a + 2, CHUNKS)
            if is_step(n):
                scores(n, a)

        def exp_chunk(n, a):
            if is_step(n):
                exponential(n, a)
                if n >= STEPS - 2 and TW:
                    bank = ps_a.tile([P, S], F32, tag="a")
                    keep_warm(bank)
                transpose_e(n, a)

        def move_x(copy, slot):
            for j in range(CHUNKS):
                transpose_x(slot, j)
            regroup_x(copy, slot)

        moved = []

        def vector_work(n, order):
            for piece in order:
                if piece == "X":
                    for slot in ([-3, -1] if n == 2 else []) + slots(n - 1):
                        quantise_x(slot)
                if piece == "V":
                    for m in projects(n - 1):
                        quantise_v(m)
                if piece == "E" and is_step(n - 2 - ELAG):
                    quantise_e(n - 2 - ELAG, 0, CHUNKS)
                if piece == "F" and ELAG == 2:
                    quantise_e(n - 3, 0, CHUNKS)
                if piece == "v":
                    for m in projects(n):
                        regroup_v(nc.vector.tensor_copy, m)
                if piece == "i":
                    for m in attends(n):
                        invert_row_sum(m)
                if piece in "012" and is_step(n - 1):
                    row_max(n - 1, int(piece), int(piece) + 1)
                if piece == "m" and is_step(n - 1):
                    row_max(n - 1, 1, 3)
                if piece == "M" and is_step(n - 1):
                    row_max(n - 1, 0, 3)
                if piece == "x" and n > 1:
                    for slot in [s for s in slots(n)[:1] if s not in moved]:
                        moved.append(slot)
                        regroup_x(nc.scalar.copy if slot >= 0 and slot % 16 in XS else nc.vector.tensor_copy, slot)
                if piece == "t" and is_step(n - 2):
                    row_max_turned(n - 2)
                if piece == "o":
                    for m in attends(n):
                        normalise_and_store(m, 0, CHUNKS)
                if piece == "q" and is_step(n + 2) and n != 1:
                    copy_qk(nc.vector.tensor_copy, n + 2)

        def dummy(count):
            for i in range(count):
                bank = ps_s.tile([P, S], F32, tag="s")
                nc.tensor.matmul(bank[:], lhsT=zeros[:, 0:P], rhs=zeros[:], start=True, stop=True)

        stack.enter_context(tc.manual_schedule())
        load_qk(0, 0, 1)
        load_mask(0)
        nc.sync.dma_start(out=mask_rows[0:B, :], in_=mask)
        if WEARLY:
            load_rows(-1)
            load_qk(0, 1, 2)
            load_qk(0, 2, H)
        else:
            load_qk(0, 1, 2)
            load_qk(0, 2, H)
            load_rows(-1)
        load_rows(0)
        load_qk(1, 0, H)
        load_mask(1)
        load_rows(1)
        dummy(NDUM[0])
        qk_t = qk_pool.tile([P, 2 * S], BF16, tag="qk_t")
        live["qk_t", 0] = qk_t
        for which, rows_sb, copy in ((0, live["q_sb", 0], nc.vector.tensor_copy), (1, live["k_sb", 0], nc.scalar.copy)):
            half_qkt = ps_two.tile([P, S], BF16, tag="w")
            for j in range(CHUNKS):
                nc.tensor.transpose(half_qkt[:, j * P : (j + 1) * P], rows_sb[:, j * DH : (j + 1) * DH], ident_bf[:])
            copy(out=qk_t[:, which * S : (which + 1) * S], in_=half_qkt[:])
        dummy(NDUM[1])
        make_mask_term(0)
        if WEARLY:
            for slot in (-4, -2)[:WE]:
                move_x(nc.vector.tensor_copy, slot)
        scores(0, 0)
        scores(0, 1)
        for j in range(CHUNKS):
            transpose_qk(1, j)
        copy_qk(nc.vector.tensor_copy, 1)
        make_mask_cols()
        for n in range(STEPS + EXP_LAG):
            if (n + 2 + DMA_LEAD) % H == 0 and 2 * H <= n + 2 + DMA_LEAD < STEPS:
                load_qk((n + 2 + DMA_LEAD) // H, 0, H)
                load_mask((n + 2 + DMA_LEAD) // H)
            if n in ROWS_AT:
                load_rows(2 + ROWS_AT.index(n))
            if is_step(n):
                squash(n, 0)
                if n == 0:
                    add_mask(nc.gpsimd if G0 else nc.vector, n, 0, 1)
            scores_ahead(n, 0)
            if 2 < n < STEPS:
                turn_back(n - 2)
            if n == STEPS:
                turn_back(n - 1)
            if n == 1:
                vector_work(n, "012")
            elif 2 < n < STEPS:
                vector_work(n, VQ1)
            if n == 2:
                for j in range(CHUNKS):
                    transpose_qk(3, j)
                copy_qk(nc.vector.tensor_copy, 3)
            if n == STEPS:
                vector_work(n, "m")
                row_max_turned(n - 1)
            if n < STEPS and not (LATEV and not slots(n)):
                for m in projects(n):
                    for j in range(CHUNKS):
                        project_v(m, j)
            exp_chunk(n - EXP_LAG, 0)
            if n >= STEPS and CT:
                exp_chunk(n - EXP_LAG, 1)
            if is_step(n - EXP_LAG - 1):
                regroup_e(nc.vector.tensor_copy if n in CV else nc.scalar.copy, n - EXP_LAG - 1, 1)
            vector_work(n, "" if n == 1 else "0" if n == 2 else "VEFi" if n == STEPS else ("F" if ELAG == 2 else "E") + "i" if n > STEPS else VQ2)
            if is_step(n):
                squash(n, 1)
                if n == STEPS - 1:
                    add_mask(nc.gpsimd, n, 0, LASTSPLIT)
                if n == 0:
                    add_mask(nc.gpsimd if G0 else nc.vector, n, 1, 2)
            scores_ahead(n, 1)
            if not (n >= STEPS and CT):
                exp_chunk(n - EXP_LAG, 1)
            if n < STEPS and LATEV and not slots(n):
                for m in projects(n):
                    for j in range(CHUNKS):
                        project_v(m, j)
            if n > 1:
                for slot in slots(n)[:1]:
                    for j in range(CHUNKS):
                        transpose_x(slot, j)
            vector_work(n, "x" if n <= 2 or n >= STEPS else VQ3)
            if n > STEPS:
                for m in attends(n - 1)[:AT]:
                    for j in range(CHUNKS):
                        attend(m, j)
            if is_step(n):
                squash(n, 2)
                if n == 0:
                    add_mask(nc.gpsimd if G0 else nc.vector, n, 2, 3)
                elif n < STEPS - 1:
                    add_mask(nc.gpsimd, n, 0, TURNED)
            scores_ahead(n, 2)
            if n == 0 and WEARLY:
                for slot in (-4, -2, -3, -1)[WE:WL]:
                    move_x(nc.vector.tensor_copy, slot)
            if n == 1:
                turn_back(0)
                row_max_turned(0)
                for slot in (-4, -2, -3, -1)[WL if WEARLY else 0:][:W3]:
                    move_x(nc.vector.tensor_copy, slot)
            else:
                if len(slots(n)) > 1:
                    vector_work(n, "x")
                for slot in slots(n)[1:]:
                    move_x(nc.scalar.copy if slot % 16 in XS else nc.vector.tensor_copy, slot)
            if n < STEPS:
                for m in attends(n):
                    for j in range(CHUNKS):
                        attend(m, j)
            if is_step(n + 2) and n != 1:
                for j in range(CHUNKS):
                    transpose_qk(n + 2, j)
            exp_chunk(n - EXP_LAG, 2)
            if n in CV0:
                regroup_e(nc.vector.tensor_copy, n - EXP_LAG, 0)
            vector_work(n, "" if n == 1 or n >= STEPS else "qmX" if n == 2 else "q" if n == 0 else VQ4)
            if n == STEPS - 1:
                if LASTSPLIT < 3:
                    add_mask(nc.vector, n, LASTSPLIT, 3)
                row_max(n, 0, 1)
            if n >= STEPS and CT:
                exp_chunk(n - EXP_LAG, 3)
            if 0 <= n - EXP_LAG and n not in CV0:
                regroup_e(nc.scalar.copy, n - EXP_LAG, 0)
            if is_step(n):
                squash(n, 3)
            scores_ahead(n, 3)
            if n == 1:
                for slot in (-4, -2, -3, -1)[WL if WEARLY else 0:][W3:]:
                    move_x(nc.vector.tensor_copy, slot)
                for slot in slots(n):
                    move_x(nc.vector.tensor_copy, slot)
            if n == STEPS - 1:
                turn_back(n - 1)
                row_max_turned(n - 1)
            if not MG and is_step(n + 1) and (n + 1) % H == 0:
                make_mask_term((n + 1) // H)
            if MG and n % H == MQ and n // H + 1 < B:
                make_mask_term(n // H + 1)
            if not (n >= STEPS and CT):
                exp_chunk(n - EXP_LAG, 3)

        last = STEPS - 1
        half = CHUNKS // 2
        regroup_e(nc.scalar.copy, last, 1)
        quantise_e(last, 0, half)
        for m in attends(STEPS)[AT:] + attends(STEPS + 1):
            for j in range(CHUNKS):
                attend(m, j)
        for a in range(half):
            attend(last, a)
        vector_work(STEPS, "o")
        invert_row_sum(last)
        if FT == 0:
            vector_work(STEPS + 1, "o")
            normalise_and_store(last, 0, half)
            quantise_e(last, half, CHUNKS)
        if FT == 1:
            quantise_e(last, half, CHUNKS)
            vector_work(STEPS + 1, "o")
        if FT == 2:
            normalise_and_store(attends(STEPS + 1)[0], 0, CHUNKS)
            normalise_and_store(last, 0, half)
            quantise_e(last, half, CHUNKS)
            normalise_and_store(attends(STEPS + 1)[1], 0, CHUNKS)
        for a in range(half, CHUNKS):
            attend(last, a)
        if FT == 1:
            normalise_and_store(last, 0, half)
        normalise_and_store(last, half, CHUNKS)
